import numpy as np
import ml_dtypes


def mxq(x, axis, fmt="e4m3"):
    dtype, down = {"e4m3": (ml_dtypes.float8_e4m3fn, 7), "e5m2": (ml_dtypes.float8_e5m2, 14)}[fmt]
    v = np.moveaxis(np.asarray(x, np.float32).astype(ml_dtypes.bfloat16).astype(np.float64), axis, -1)
    blocks = v.reshape(v.shape[:-1] + (-1, 32))
    amax = np.abs(blocks).max(-1, keepdims=True)
    byte = np.maximum(np.where(amax > 0, np.frexp(amax)[1] - 1 + 127, 0) - down, 1)
    scale = np.exp2(byte - 127.0)
    codes = (blocks / scale).astype(np.float32).astype(dtype).astype(np.float64)
    return np.moveaxis((codes * scale).reshape(v.shape), -1, axis)


WIDE = False


def mx_kscale(k):
    if not WIDE:
        return np.ones(k)
    levels = np.array([18, -18])
    if k % 512:
        return np.exp2(np.random.permutation(np.resize(levels, k // 32))).repeat(32)
    a = np.empty((k // 512, 16))
    for p in range(k // 512):
        a[p, :8] = np.random.permutation(np.resize(levels, 8))
        for g in range(8):
            far = levels[np.abs(levels - a[p, g]) >= 10]
            a[p, g + 8] = far[np.random.randint(len(far))]
    return np.exp2(a.ravel()).repeat(32)


BF16 = ml_dtypes.bfloat16


def bf(x):
    return np.asarray(x, np.float32).astype(BF16)


def f64(x):
    return np.asarray(x).astype(np.float64)


B, S, F, H, D = 4, 256, 1024, 8, 128
THETA = 10000.0
HD = H * D
T = B * S


def rope_tables():
    freqs = 1.0 / THETA ** (f64(np.arange(0, D, 2)) / D)
    ang = np.outer(f64(np.arange(S)), freqs)
    ang = np.concatenate((ang, ang), axis=-1)
    return np.cos(ang), np.sin(ang)


def rotate_half(v):
    v1, v2 = v[..., : D // 2], v[..., D // 2 :]
    return np.concatenate((-v2, v1), axis=-1)


def rotate_half_back(v):
    v1, v2 = v[..., : D // 2], v[..., D // 2 :]
    return np.concatenate((v2, -v1), axis=-1)


def rope_back(g, cos, sin):
    return g * cos + rotate_half_back(g * sin)


def setup_inputs():
    s = mx_kscale(T).reshape(B, S)
    u = mx_kscale(HD).reshape(2, H, D // 2)
    u = np.concatenate((u, u), axis=-1)
    uq, uk = u[0], u[1]
    x = bf(np.random.standard_normal((B, S, F)) * s[:, :, None])
    wq = bf(np.random.standard_normal((F, H, D)) / np.sqrt(F) / uq[None])
    bq = bf(np.random.standard_normal((H, D)) * 0.3)
    wk = bf(np.random.standard_normal((F, H, D)) / np.sqrt(F) / uk[None])
    bk = bf(np.random.standard_normal((H, D)) * 0.3)
    g0 = bf(np.random.standard_normal((B, S, H, D)) * np.exp2(np.random.randint(-6, 1, (B, S, 1, 1))) / s[:, :, None, None] * uq)
    g1 = bf(np.random.standard_normal((B, S, H, D)) * np.exp2(np.random.randint(-6, 1, (B, S, 1, 1))) / s[:, :, None, None] * uk)
    return {"x": x, "wq": wq, "bq": bq, "wk": wk, "bk": bk, "grad_0": g0, "grad_1": g1}


def reference(x, wq, bq, wk, bk, grad_0, grad_1):
    cos, sin = rope_tables()
    cos, sin = cos[None, :, None, :], sin[None, :, None, :]
    dq = rope_back(f64(grad_0), cos, sin).reshape(T, HD)
    dk = rope_back(f64(grad_1), cos, sin).reshape(T, HD)
    dz = np.concatenate((dq, dk), axis=1)
    w = np.concatenate((f64(wq).reshape(F, HD), f64(wk).reshape(F, HD)), axis=1)
    dx = mxq(dz, 1, "e5m2") @ mxq(w, 1, "e4m3").T
    xt = mxq(f64(x).reshape(T, F), 0, "e4m3")
    dw = xt.T @ mxq(dz, 0, "e5m2")
    dwq = dw[:, :HD].reshape(F, H, D)
    dwk = dw[:, HD:].reshape(F, H, D)
    return dx.reshape(B, S, F), dwq, dwk

@@ -1,0 +1,350 @@
+import math
+from contextlib import ExitStack
+
+import concourse.mybir as mybir
+from concourse.masks import make_identity
+
+F32 = mybir.dt.float32
+BF16 = mybir.dt.bfloat16
+I32 = mybir.dt.int32
+U32 = mybir.dt.uint32
+U8 = mybir.dt.uint8
+E4 = mybir.dt.float8_e4m3fn_x4
+E5 = mybir.dt.float8_e5m2_x4
+ALU = mybir.AluOpType
+ACT = mybir.ActivationFunctionType
+
+P = 128
+T, F, HD = 1024, 1024, 1024
+THETA = 10000.0
+FLOPS = 2 * 2 * T * F * 2 * HD
+BYTES = 2 * (T * F + 2 * F * HD + 2 * T * HD) + 4 * (T * F + 2 * F * HD)
+
+GPS_ADDS = 7
+
+
+def tile_selfattention_pa_v_kernel(tc, x, wq, bq, wk, bk, grad_0, grad_1, out_0, out_1, out_2):
+    nc = tc.nc
+    xf = x.rearrange("b s f -> (b s) f").rearrange("(g p j) f -> g p j f", p=P, j=4)
+    gf = [a.rearrange("b s h d -> (b s) (h d)").rearrange("(g p j) c -> g p j c", p=P, j=4) for a in (grad_0, grad_1)]
+    wf = [a.rearrange("f h d -> f (h d)").rearrange("(z a p) c -> z p a c", z=2, p=P) for a in (wq, wk)]
+    o0 = out_0.rearrange("b s f -> (b s) f").rearrange("(g p j) f -> g j p f", p=P, j=4)
+    ow = [a.rearrange("f h d -> f (h d)").rearrange("(m p) c -> m p c", p=P) for a in (out_1, out_2)]
+
+    with ExitStack() as ctx:
+        const = ctx.enter_context(tc.tile_pool(name="const", bufs=1))
+        inp = ctx.enter_context(tc.tile_pool(name="inp", bufs=1))
+        keep = ctx.enter_context(tc.tile_pool(name="keep", bufs=1))
+        work = ctx.enter_context(tc.tile_pool(name="work", bufs=2))
+        outs = ctx.enter_context(tc.tile_pool(name="outs", bufs=6))
+        ptab = ctx.enter_context(tc.psum_pool(name="ptab", bufs=1))
+        ptr = ctx.enter_context(tc.psum_pool(name="ptr", bufs=3))
+        pmm = ctx.enter_context(tc.psum_pool(name="pmm", bufs=4))
+        ctx.enter_context(tc.manual_schedule())
+
+        gt = {}
+
+        def load_q(g, k):
+            t = inp.tile([P, 4, 512], BF16, name=f"gq{g}{k}", align_bytes=64)
+            nc.sync.dma_start(out=t[:], in_=gf[0][g][:, :, 512 * k : 512 * k + 512])
+            gt[g, k] = t
+
+        def load_k(g):
+            t = inp.tile([P, 4, 1024], BF16, name=f"xg{g}", align_bytes=64)
+            nc.sync.dma_start(out=t[:], in_=gf[1][g])
+            gt[g, 2] = t[:, :, 0:512]
+            gt[g, 3] = t[:, :, 512:1024]
+
+        xt = []
+
+        def load_x(g):
+            t = inp.tile([P, 4, 1024], BF16, name=f"xg{g}", align_bytes=64)
+            nc.sync.dma_start(out=t[:], in_=xf[g])
+            xt.append(t)
+
+        wt = {}
+
+        def load_w(l, z):
+            t = inp.tile([P, 4, 1024], BF16, name=f"w{z}", align_bytes=64)
+            nc.sync.dma_start(out=t[:], in_=wf[l][z])
+            wt[l, z] = t
+
+        load_q(0, 0)
+        load_q(1, 0)
+        load_x(0)
+        load_x(1)
+        load_q(0, 1)
+        load_q(1, 1)
+        load_w(0, 0)
+        load_w(0, 1)
+
+        qi = const.tile([P, 1], I32)
+        nc.gpsimd.iota(qi[:], pattern=[[0, 1]], base=0, channel_multiplier=1)
+        pos = const.tile([P, 256], F32)
+        nc.gpsimd.iota(pos[:], pattern=[[1, 4], [4, 64]], base=0, channel_multiplier=0, allow_small_or_imprecise_dtypes=True)
+        ident = const.tile([P, P], F32)
+        make_identity(nc, ident[:])
+        bits = const.tile([P, 7], I32)
+        for b in range(7):
+            nc.vector.tensor_scalar(out=bits[:, b : b + 1], in0=qi[:], scalar1=b, scalar2=1, op0=ALU.logical_shift_right, op1=ALU.bitwise_and)
+        fac = const.tile([P, 6], F32)
+        for b in range(6):
+            r = THETA ** (-(2.0**b) / 64.0)
+            nc.vector.tensor_scalar(out=fac[:, b : b + 1], in0=bits[:, b : b + 1], scalar1=r - 1.0, scalar2=1.0, op0=ALU.mult, op1=ALU.add)
+        phase = const.tile([P, 1], F32)
+        nc.vector.tensor_scalar(out=phase[:], in0=bits[:, 6:7], scalar1=-0.25, scalar2=0.25, op0=ALU.mult, op1=ALU.add)
+        fac3 = const.tile([P, 3], F32)
+        nc.vector.tensor_tensor(out=fac3[:], in0=fac[:, 0:3], in1=fac[:, 3:6], op=ALU.mult)
+        fac2 = const.tile([P, 1], F32)
+        nc.vector.tensor_tensor(out=fac2[:], in0=fac3[:, 0:1], in1=fac3[:, 1:2], op=ALU.mult)
+        freq = const.tile([P, 1], F32)
+        nc.vector.scalar_tensor_tensor(out=freq[:], in0=fac2[:], scalar=0.5 / math.pi, in1=fac3[:, 2:3], op0=ALU.mult, op1=ALU.mult)
+        turns = const.tile([P, 256], F32)
+        nc.vector.tensor_scalar(out=turns[:], in0=pos[:], scalar1=freq[:], scalar2=phase[:], op0=ALU.mult, op1=ALU.add)
+        whole = const.tile([P, 256], I32)
+        nc.vector.tensor_copy(out=whole[:], in_=turns[:])
+        rest = const.tile([P, 4, 64], F32)
+        nc.vector.tensor_tensor(out=rest[:].rearrange("p t s -> p (t s)"), in0=turns[:], in1=whole[:], op=ALU.subtract)
+        wave = const.tile([P, 4, 2, 64], F32)
+        nc.scalar.activation(out=wave[:], in_=rest[:].unsqueeze(2).to_broadcast([P, 4, 2, 64]), func=ACT.Sin, scale=2.0 * math.pi)
+        tab = ptab.tile([P, 4, P], F32)
+        for t in range(4):
+            nc.tensor.transpose(tab[:, t, :], wave[:, t, :, :].rearrange("p a s -> p (a s)"), ident[:])
+        cosb = tab[:, :, 0:64].unsqueeze(2).to_broadcast([P, 4, 4, 64])
+        sinb = tab[:, :, 64:128].unsqueeze(2).to_broadcast([P, 4, 4, 64])
+
+        AB, DZ, ROW, DZT, COL = {}, {}, {}, {}, {}
+        banks = {}
+
+        def source(u, hh):
+            return gt[u][:, :, 256 * hh : 256 * hh + 256].rearrange("p t (q j) -> p t q j", j=64)
+
+        def mult_a(u, hh):
+            a = work.tile([P, 4, 4, 64], F32, name="prod_a", bufs=4, align_bytes=64)
+            nc.vector.tensor_tensor(out=a[:], in0=source(u, hh), in1=cosb, op=ALU.mult)
+            AB[u, hh] = [a]
+
+        def mult_b(u, hh):
+            b = work.tile([P, 4, 4, 64], F32, name="prod_b", bufs=4, align_bytes=64)
+            nc.vector.tensor_tensor(out=b[:], in0=source(u, hh), in1=sinb, op=ALU.mult)
+            AB[u, hh].append(b)
+
+
+        def adds(u, hh, gps, share=GPS_ADDS):
+            if u not in DZ:
+                dz = work.tile([P, 512, 4], BF16, name="dz", bufs=1, align_bytes=64)
+                DZ[u] = dz
+            a, b = AB[u, hh]
+            for head in range(2):
+                for half in range(2):
+                    n = 4 * hh + 2 * head + half
+                    on_gps = (n * share) // 8 != ((n + 1) * share) // 8
+                    if on_gps != gps:
+                        continue
+                    eng = nc.gpsimd if on_gps else nc.vector
+                    c0 = 256 * hh + 128 * head + 64 * half
+                    eng.tensor_tensor(
+                        out=DZ[u][:, c0 : c0 + 64, :].rearrange("p (c i) t -> p c t i", i=4),
+                        in0=a[:, :, 2 * head + half, :].rearrange("p t (c i) -> p c t i", i=4),
+                        in1=b[:, :, 2 * head + 1 - half, :].rearrange("p t (c i) -> p c t i", i=4),
+                        op=ALU.subtract if half else ALU.add,
+                    )
+
+        def quant(dst, src, width, fmt, key, name):
+            codes = keep.tile([P, width], U32, name=f"{name}c", align_bytes=64)
+            scales = keep.tile([P, width], U8, name=f"{name}s", align_bytes=64)
+            nc.vector.quantize_mx(out=codes[:].bitcast(fmt), scales=scales[:], in_=src)
+            dst[key] = (codes, scales)
+
+        def quant_row(u):
+            quant(ROW, DZ[u][:].rearrange("p c t -> p (c t)"), 512, E5, u, f"r{u[0]}{u[1]}")
+
+        def transpose_dz(u):
+            words = DZ[u][:].rearrange("p c t -> p (c t)").bitcast(F32)
+            for tp in range(2):
+                bank = ptr.tile([P, 4, P], F32, name="tr")
+                for t in range(4):
+                    nc.tensor.transpose(bank[:, t, :], words[:, 2 * t + tp : 1024 : 8], ident[:])
+                banks[u, tp] = bank
+
+        def copy_dz(u, vec=False):
+            dzt = work.tile([P, 512, 4], BF16, name="dzt", bufs=2, align_bytes=64)
+            for tp in range(2):
+                copy = nc.vector.tensor_copy if vec and tp == 1 else nc.scalar.copy
+                copy(
+                    out=dzt[:, 256 * tp : 256 * tp + 256, :].rearrange("i (e p) t -> i e p t", e=2),
+                    in_=banks[u, tp][:].rearrange("i t p -> i (t p)").bitcast(BF16).rearrange("i (t p e) -> i e p t", t=4, e=2),
+                )
+            DZT[u] = dzt
+
+        def quant_col(u):
+            quant(COL, DZT[u][:].rearrange("p c t -> p (c t)"), 512, E5, u, f"c{u[0]}{u[1]}")
+
+        XI, XQ = {}, {}
+
+        def copy_x(g, h, gps):
+            xi = work.tile([P, 512, 4], BF16, name="xi", bufs=4, align_bytes=64)
+            dst = xi[:].rearrange("p (c i) t -> p c t i", i=4)
+            src = xt[g][:, :, 512 * h : 512 * h + 512].rearrange("p t (c i) -> p c t i", i=4)
+            if gps:
+                nc.gpsimd.tensor_scalar(out=dst, in0=src, scalar1=1.0, scalar2=0.0, op0=ALU.mult, op1=ALU.add)
+            else:
+                nc.scalar.copy(out=dst, in_=src)
+            XI[g, h] = xi
+
+        def quant_x(g, h):
+            quant(XQ, XI[g, h][:].rearrange("p c t -> p (c t)"), 512, E4, (g, h), f"x{g}{h}")
+
+        WT, WQ = {}, {}
+
+        def transpose_w(k, z):
+            words = wt[k // 2, z][:].rearrange("p a c -> p (a c)").bitcast(F32)
+            for y in range(2):
+                bank = ptr.tile([P, 2, 2, P], F32, name="tr")
+                for a in range(2):
+                    for u in range(2):
+                        s = 512 * (2 * y + a) + 256 * (k % 2)
+                        nc.tensor.transpose(bank[:, a, u, :], words[:, s + u : s + 256 : 2], ident[:])
+                banks["w", k, z, y] = bank
+
+        def copy_w(k, z):
+            wtt = work.tile([P, 512, 4], BF16, name="wtt", bufs=2, align_bytes=64)
+            wwords = wtt[:].rearrange("p c t -> p (c t)").bitcast(F32)
+            for y in range(2):
+                nc.scalar.copy(
+                    out=wwords[:, 512 * y : 512 * y + 512].rearrange("i (a r u) -> i a r u", a=2, u=2),
+                    in_=banks["w", k, z, y][:].rearrange("i a u r -> i a r u"),
+                )
+            WT[k, z] = wtt
+
+        def quant_w(k, z):
+            quant(WQ, WT[k, z][:].rearrange("p c t -> p (c t)"), 512, E4, (k, z), f"w{k}{z}")
+
+        def mx(bank, lhs, lcol, lfmt, rhs, rfmt, start, stop):
+            nc.tensor.matmul_mx(
+                out=bank[:],
+                lhsT=lhs[0][:, lcol : lcol + P].bitcast(lfmt),
+                lhsT_scale=lhs[1][:, lcol : lcol + P],
+                rhs=rhs[0][:].bitcast(rfmt),
+                rhs_scale=rhs[1][:],
+                start=start,
+                stop=stop,
+            )
+
+        count = [0]
+
+        def evac(dst, bank, vec):
+            if vec:
+                nc.vector.tensor_copy(out=dst, in_=bank[:])
+            else:
+                nc.scalar.copy(out=dst, in_=bank[:])
+
+        def dw_pair(k, m2, vecs):
+            ot = outs.tile([P, 2, 512], F32, name="ot")
+            for a in range(2):
+                m = 2 * m2 + a
+                bank = pmm.tile([P, 512], F32, name="mm")
+                for g in range(2):
+                    mx(bank, XQ[g, m // 4], 128 * (m % 4), E4, ROW[g, k], E5, g == 0, g == 1)
+                evac(ot[:, a, :], bank, vecs[a])
+            nc.sync.dma_start(
+                out=ow[k // 2][2 * m2 : 2 * m2 + 2, :, 512 * (k % 2) : 512 * (k % 2) + 512].rearrange("a p c -> p a c"),
+                in_=ot[:],
+            )
+
+        def dx_open(g, t, z, pool=pmm):
+            return pool.tile([P, 512], F32, name="mm" if pool is pmm else "tr")
+
+        def dx_pass(bank, g, t, z, ks):
+            for k in ks:
+                mx(bank, COL[g, k], 128 * t, E5, WQ[k, z], E4, k == 0, k == 3)
+
+        OPEN = {}
+
+        def dx_early(g, t, ks):
+            for z in range(2):
+                if (g, t, z) not in OPEN:
+                    OPEN[g, t, z] = dx_open(g, t, z)
+                dx_pass(OPEN[g, t, z], g, t, z, ks)
+
+        def dx_pair(g, t, vecs, pool=pmm):
+            ot = outs.tile([P, 2, 512], F32, name="ot")
+            for z in range(2):
+                if (g, t, z) in OPEN:
+                    bank = OPEN[g, t, z]
+                    dx_pass(bank, g, t, z, (3,))
+                else:
+                    bank = dx_open(g, t, z, pool)
+                    dx_pass(bank, g, t, z, (0, 1, 2, 3))
+                evac(ot[:, z, :], bank, vecs[z])
+            nc.sync.dma_start(out=o0[g][t], in_=ot[:].rearrange("p z f -> p (z f)"))
+
+        U = [(0, 0), (1, 0), (0, 1), (0, 2), (0, 3), (1, 1), (1, 2), (1, 3)]
+        todo = {}
+
+        def at(h, part, *calls):
+            todo.setdefault((h, part), []).extend(calls)
+
+        def later(fn, *args):
+            return lambda: fn(*args)
+
+        def play(s, part):
+            for call in todo.pop((s, part), []):
+                call()
+
+        SS = (False, False)
+        SV = (False, True)
+        at(0, "W", later(copy_x, 0, 0, True), later(copy_x, 0, 1, True))
+        at(0, "X", later(copy_x, 1, 0, False))
+        at(1, "Q", later(quant_x, 0, 0), later(quant_x, 0, 1))
+        at(1, "X", later(copy_x, 1, 1, False))
+        at(2, "Q", later(quant_x, 1, 0), later(quant_x, 1, 1))
+        at(0, "X", later(load_k, 0))
+        wj = [(0, 0), (1, 0), (0, 1), (1, 1), (2, 0), (3, 0), (2, 1), (3, 1)]
+        for n in range(8):
+            s = (1, 1, 2, 2, 3, 3, 4, 4)[n]
+            at(s, "X", later(transpose_w, *wj[n]), later(copy_w, *wj[n]))
+            at(s + 1, "Q", later(quant_w, *wj[n]))
+        at(1, "X", later(load_w, 1, 0), later(load_k, 1))
+        at(2, "X", later(load_w, 1, 1))
+        for n in range(4):
+            at(2, "X", later(dw_pair, 0, n, SS))
+        for n in range(2):
+            at(5, "X", later(dx_early, 0, n, (0, 1, 2)))
+        for n in range(4):
+            at(6, "X", later(dx_pair, 0, n, SS))
+        for n in range(4):
+            at(7, "X", later(dw_pair, 1, n, SS))
+
+        for s in range(8):
+            for hh in range(2):
+                mult_a(U[s], hh)
+                mult_b(U[s], hh)
+            if s >= 1:
+                adds(U[s - 1], 0, True)
+                adds(U[s - 1], 1, True)
+            play(s, "W")
+            if s >= 1:
+                adds(U[s - 1], 0, False)
+                adds(U[s - 1], 1, False)
+            if s >= 2:
+                quant_col(U[s - 2])
+            play(s, "Q")
+            if s >= 1:
+                transpose_dz(U[s - 1])
+                copy_dz(U[s - 1])
+                quant_row(U[s - 1])
+            play(s, "X")
+        adds(U[7], 0, False, 0)
+        adds(U[7], 1, False, 0)
+        transpose_dz(U[7])
+        quant_row(U[7])
+        copy_dz(U[7], True)
+        quant_col(U[6])
+        quant_col(U[7])
+        for m2 in range(4):
+            dw_pair(2, m2, SV)
+        for t in range(4):
+            dx_pair(1, t, SV)
+        for m2 in range(4):
+            dw_pair(3, m2, SV)

@@ -20,7 +20,7 @@ THETA = 10000.0
 FLOPS = 2 * 2 * T * F * 2 * HD
 BYTES = 2 * (T * F + 2 * F * HD + 2 * T * HD) + 4 * (T * F + 2 * F * HD)
 
-GPS_ADDS = 7
+GPS_COLS = 448
 
 
 def tile_selfattention_pa_v_kernel(tc, x, wq, bq, wk, bk, grad_0, grad_1, out_0, out_1, out_2):
@@ -38,11 +38,11 @@ def tile_selfattention_pa_v_kernel(tc, x, wq, bq, wk, bk, grad_0, grad_1, out_0,
         work = ctx.enter_context(tc.tile_pool(name="work", bufs=2))
         outs = ctx.enter_context(tc.tile_pool(name="outs", bufs=6))
         ptab = ctx.enter_context(tc.psum_pool(name="ptab", bufs=1))
-        ptr = ctx.enter_context(tc.psum_pool(name="ptr", bufs=3))
+        ptr = ctx.enter_context(tc.psum_pool(name="ptr", bufs=2))
         pmm = ctx.enter_context(tc.psum_pool(name="pmm", bufs=4))
         ctx.enter_context(tc.manual_schedule())
 
-        gt = {}
+        gt, xt, wt = {}, {}, {}
 
         def load_q(g, k):
             t = inp.tile([P, 4, 512], BF16, name=f"gq{g}{k}", align_bytes=64)
@@ -55,14 +55,10 @@ def tile_selfattention_pa_v_kernel(tc, x, wq, bq, wk, bk, grad_0, grad_1, out_0,
             gt[g, 2] = t[:, :, 0:512]
             gt[g, 3] = t[:, :, 512:1024]
 
-        xt = []
-
         def load_x(g):
             t = inp.tile([P, 4, 1024], BF16, name=f"xg{g}", align_bytes=64)
             nc.sync.dma_start(out=t[:], in_=xf[g])
-            xt.append(t)
-
-        wt = {}
+            xt[g] = t
 
         def load_w(l, z):
             t = inp.tile([P, 4, 1024], BF16, name=f"w{z}", align_bytes=64)
@@ -70,13 +66,13 @@ def tile_selfattention_pa_v_kernel(tc, x, wq, bq, wk, bk, grad_0, grad_1, out_0,
             wt[l, z] = t
 
         load_q(0, 0)
-        load_q(1, 0)
         load_x(0)
+        load_q(1, 0)
         load_x(1)
         load_q(0, 1)
-        load_q(1, 1)
         load_w(0, 0)
         load_w(0, 1)
+        load_q(1, 1)
 
         qi = const.tile([P, 1], I32)
         nc.gpsimd.iota(qi[:], pattern=[[0, 1]], base=0, channel_multiplier=1)
@@ -105,59 +101,45 @@ def tile_selfattention_pa_v_kernel(tc, x, wq, bq, wk, bk, grad_0, grad_1, out_0,
         nc.vector.tensor_copy(out=whole[:], in_=turns[:])
         rest = const.tile([P, 4, 64], F32)
         nc.vector.tensor_tensor(out=rest[:].rearrange("p t s -> p (t s)"), in0=turns[:], in1=whole[:], op=ALU.subtract)
-        wave = const.tile([P, 4, 2, 64], F32)
-        nc.scalar.activation(out=wave[:], in_=rest[:].unsqueeze(2).to_broadcast([P, 4, 2, 64]), func=ACT.Sin, scale=2.0 * math.pi)
-        tab = ptab.tile([P, 4, P], F32)
-        for t in range(4):
-            nc.tensor.transpose(tab[:, t, :], wave[:, t, :, :].rearrange("p a s -> p (a s)"), ident[:])
-        cosb = tab[:, :, 0:64].unsqueeze(2).to_broadcast([P, 4, 4, 64])
-        sinb = tab[:, :, 64:128].unsqueeze(2).to_broadcast([P, 4, 4, 64])
+        tabs = []
+        for sign in (1.0, -1.0):
+            wave = const.tile([P, 4, 2, 64], F32, name="wave", bufs=2)
+            nc.scalar.activation(out=wave[:], in_=rest[:].unsqueeze(2).to_broadcast([P, 4, 2, 64]), func=ACT.Sin, scale=sign * 2.0 * math.pi)
+            tab = ptab.tile([P, 4, P], F32, name="tab" if sign > 0 else "neg")
+            for t in range(4):
+                nc.tensor.transpose(tab[:, t, :], wave[:, t, :, :].rearrange("p a s -> p (a s)"), ident[:])
+            tabs.append(tab)
+        cos = tabs[0][:, :, 0:64].unsqueeze(2)
+        sin = tabs[0][:, :, 64:128].unsqueeze(2)
+        nsin = tabs[1][:, :, 64:128].unsqueeze(2)
 
         AB, DZ, ROW, DZT, COL = {}, {}, {}, {}, {}
         banks = {}
 
-        def source(u, hh):
-            return gt[u][:, :, 256 * hh : 256 * hh + 256].rearrange("p t (q j) -> p t q j", j=64)
+        def mult(u):
+            src = gt[u][:].rearrange("p t (q j) -> p t q j", j=64)
+            a = work.tile([P, 4, 8, 64], F32, name="prod_a", align_bytes=64)
+            nc.vector.tensor_tensor(out=a[:], in0=src, in1=cos.to_broadcast([P, 4, 8, 64]), op=ALU.mult)
+            b = work.tile([P, 4, 8, 64], F32, name="prod_b", align_bytes=64)
+            nc.vector.tensor_tensor(out=b[:, :, 0:8:2, :], in0=src[:, :, 1:8:2, :], in1=sin.to_broadcast([P, 4, 4, 64]), op=ALU.mult)
+            nc.vector.tensor_tensor(out=b[:, :, 1:8:2, :], in0=src[:, :, 0:8:2, :], in1=nsin.to_broadcast([P, 4, 4, 64]), op=ALU.mult)
+            AB[u] = (a, b)
 
-        def mult_a(u, hh):
-            a = work.tile([P, 4, 4, 64], F32, name="prod_a", bufs=4, align_bytes=64)
-            nc.vector.tensor_tensor(out=a[:], in0=source(u, hh), in1=cosb, op=ALU.mult)
-            AB[u, hh] = [a]
-
-        def mult_b(u, hh):
-            b = work.tile([P, 4, 4, 64], F32, name="prod_b", bufs=4, align_bytes=64)
-            nc.vector.tensor_tensor(out=b[:], in0=source(u, hh), in1=sinb, op=ALU.mult)
-            AB[u, hh].append(b)
-
-
-        def adds(u, hh, gps, share=GPS_ADDS):
+        def add(u, eng, lo, hi):
             if u not in DZ:
                 dz = work.tile([P, 512, 4], BF16, name="dz", bufs=1, align_bytes=64)
                 DZ[u] = dz
-            a, b = AB[u, hh]
-            for head in range(2):
-                for half in range(2):
-                    n = 4 * hh + 2 * head + half
-                    on_gps = (n * share) // 8 != ((n + 1) * share) // 8
-                    if on_gps != gps:
-                        continue
-                    eng = nc.gpsimd if on_gps else nc.vector
-                    c0 = 256 * hh + 128 * head + 64 * half
-                    eng.tensor_tensor(
-                        out=DZ[u][:, c0 : c0 + 64, :].rearrange("p (c i) t -> p c t i", i=4),
-                        in0=a[:, :, 2 * head + half, :].rearrange("p t (c i) -> p c t i", i=4),
-                        in1=b[:, :, 2 * head + 1 - half, :].rearrange("p t (c i) -> p c t i", i=4),
-                        op=ALU.subtract if half else ALU.add,
-                    )
+            a, b = [s[:].rearrange("p t q j -> p t (q j)")[:, :, lo:hi].rearrange("p t (c i) -> p c t i", i=4) for s in AB[u]]
+            eng.tensor_tensor(out=DZ[u][:, lo:hi, :].rearrange("p (c i) t -> p c t i", i=4), in0=a, in1=b, op=ALU.add)
 
-        def quant(dst, src, width, fmt, key, name):
-            codes = keep.tile([P, width], U32, name=f"{name}c", align_bytes=64)
-            scales = keep.tile([P, width], U8, name=f"{name}s", align_bytes=64)
-            nc.vector.quantize_mx(out=codes[:].bitcast(fmt), scales=scales[:], in_=src)
+        def quant(dst, src, fmt, key, name):
+            codes = keep.tile([P, 512], U32, name=f"{name}c", align_bytes=64)
+            scales = keep.tile([P, 512], U8, name=f"{name}s", align_bytes=64)
+            nc.vector.quantize_mx(out=codes[:].bitcast(fmt), scales=scales[:], in_=src[:].rearrange("p c t -> p (c t)"))
             dst[key] = (codes, scales)
 
         def quant_row(u):
-            quant(ROW, DZ[u][:].rearrange("p c t -> p (c t)"), 512, E5, u, f"r{u[0]}{u[1]}")
+            quant(ROW, DZ[u], E5, u, f"r{u[0]}{u[1]}")
 
         def transpose_dz(u):
             words = DZ[u][:].rearrange("p c t -> p (c t)").bitcast(F32)
@@ -178,22 +160,20 @@ def tile_selfattention_pa_v_kernel(tc, x, wq, bq, wk, bk, grad_0, grad_1, out_0,
             DZT[u] = dzt
 
         def quant_col(u):
-            quant(COL, DZT[u][:].rearrange("p c t -> p (c t)"), 512, E5, u, f"c{u[0]}{u[1]}")
+            quant(COL, DZT[u], E5, u, f"c{u[0]}{u[1]}")
 
         XI, XQ = {}, {}
 
-        def copy_x(g, h, gps):
-            xi = work.tile([P, 512, 4], BF16, name="xi", bufs=4, align_bytes=64)
-            dst = xi[:].rearrange("p (c i) t -> p c t i", i=4)
-            src = xt[g][:, :, 512 * h : 512 * h + 512].rearrange("p t (c i) -> p c t i", i=4)
-            if gps:
-                nc.gpsimd.tensor_scalar(out=dst, in0=src, scalar1=1.0, scalar2=0.0, op0=ALU.mult, op1=ALU.add)
-            else:
-                nc.scalar.copy(out=dst, in_=src)
+        def copy_x(g, h):
+            xi = work.tile([P, 512, 4], BF16, name="stage", bufs=4, align_bytes=64)
+            nc.scalar.copy(
+                out=xi[:].rearrange("p (c i) t -> p c t i", i=4),
+                in_=xt[g][:, :, 512 * h : 512 * h + 512].rearrange("p t (c i) -> p c t i", i=4),
+            )
             XI[g, h] = xi
 
         def quant_x(g, h):
-            quant(XQ, XI[g, h][:].rearrange("p c t -> p (c t)"), 512, E4, (g, h), f"x{g}{h}")
+            quant(XQ, XI[g, h], E4, (g, h), f"x{g}{h}")
 
         WT, WQ = {}, {}
 
@@ -208,7 +188,7 @@ def tile_selfattention_pa_v_kernel(tc, x, wq, bq, wk, bk, grad_0, grad_1, out_0,
                 banks["w", k, z, y] = bank
 
         def copy_w(k, z):
-            wtt = work.tile([P, 512, 4], BF16, name="wtt", bufs=2, align_bytes=64)
+            wtt = work.tile([P, 512, 4], BF16, name="stage", bufs=4, align_bytes=64)
             wwords = wtt[:].rearrange("p c t -> p (c t)").bitcast(F32)
             for y in range(2):
                 nc.scalar.copy(
@@ -218,7 +198,7 @@ def tile_selfattention_pa_v_kernel(tc, x, wq, bq, wk, bk, grad_0, grad_1, out_0,
             WT[k, z] = wtt
 
         def quant_w(k, z):
-            quant(WQ, WT[k, z][:].rearrange("p c t -> p (c t)"), 512, E4, (k, z), f"w{k}{z}")
+            quant(WQ, WT[k, z], E4, (k, z), f"w{k}{z}")
 
         def mx(bank, lhs, lcol, lfmt, rhs, rfmt, start, stop):
             nc.tensor.matmul_mx(
@@ -231,19 +211,26 @@ def tile_selfattention_pa_v_kernel(tc, x, wq, bq, wk, bk, grad_0, grad_1, out_0,
                 stop=stop,
             )
 
-        count = [0]
-
         def evac(dst, bank, vec):
             if vec:
                 nc.vector.tensor_copy(out=dst, in_=bank[:])
             else:
                 nc.scalar.copy(out=dst, in_=bank[:])
 
+        SPOTS = [(pmm, "mm")]
+        turn = [0]
+
+        def new_bank():
+            pool, name = SPOTS[turn[0] % len(SPOTS)]
+            turn[0] += 1
+            bank = pool.tile([P, 512], F32, name=name)
+            return bank
+
         def dw_pair(k, m2, vecs):
             ot = outs.tile([P, 2, 512], F32, name="ot")
             for a in range(2):
                 m = 2 * m2 + a
-                bank = pmm.tile([P, 512], F32, name="mm")
+                bank = new_bank()
                 for g in range(2):
                     mx(bank, XQ[g, m // 4], 128 * (m % 4), E4, ROW[g, k], E5, g == 0, g == 1)
                 evac(ot[:, a, :], bank, vecs[a])
@@ -252,99 +239,101 @@ def tile_selfattention_pa_v_kernel(tc, x, wq, bq, wk, bk, grad_0, grad_1, out_0,
                 in_=ot[:],
             )
 
-        def dx_open(g, t, z, pool=pmm):
-            return pool.tile([P, 512], F32, name="mm" if pool is pmm else "tr")
+        OPEN, PART = {}, {}
 
-        def dx_pass(bank, g, t, z, ks):
+        def dx_pass(bank, g, t, z, ks, first, last):
             for k in ks:
-                mx(bank, COL[g, k], 128 * t, E5, WQ[k, z], E4, k == 0, k == 3)
+                mx(bank, COL[g, k], 128 * t, E5, WQ[k, z], E4, k == first, k == last)
 
-        OPEN = {}
-
-        def dx_early(g, t, ks):
+        def dx_open(g, t, ks):
             for z in range(2):
-                if (g, t, z) not in OPEN:
-                    OPEN[g, t, z] = dx_open(g, t, z)
-                dx_pass(OPEN[g, t, z], g, t, z, ks)
+                bank = new_bank()
+                OPEN[g, t, z] = bank
+                dx_pass(bank, g, t, z, ks, ks[0], 3)
 
-        def dx_pair(g, t, vecs, pool=pmm):
+        def dx_part(g, t, vecs):
+            part = outs.tile([P, 2, 512], F32, name=f"part{g}{t}", bufs=1)
+            for z in range(2):
+                bank = new_bank()
+                dx_pass(bank, g, t, z, (0, 1), 0, 1)
+                evac(part[:, z, :], bank, vecs[z])
+            PART[g, t] = part
+
+        def dx_pair(g, t, vecs):
             ot = outs.tile([P, 2, 512], F32, name="ot")
+            part = PART.get((g, t))
             for z in range(2):
                 if (g, t, z) in OPEN:
                     bank = OPEN[g, t, z]
-                    dx_pass(bank, g, t, z, (3,))
+                    dx_pass(bank, g, t, z, (3,), -1, 3)
                 else:
-                    bank = dx_open(g, t, z, pool)
-                    dx_pass(bank, g, t, z, (0, 1, 2, 3))
-                evac(ot[:, z, :], bank, vecs[z])
+                    bank = new_bank()
+                    dx_pass(bank, g, t, z, (2, 3) if part is not None else (0, 1, 2, 3), 2 if part is not None else 0, 3)
+                if part is not None:
+                    nc.vector.tensor_tensor(out=ot[:, z, :], in0=bank[:], in1=part[:, z, :], op=ALU.add)
+                else:
+                    evac(ot[:, z, :], bank, vecs[z])
             nc.sync.dma_start(out=o0[g][t], in_=ot[:].rearrange("p z f -> p (z f)"))
 
-        U = [(0, 0), (1, 0), (0, 1), (0, 2), (0, 3), (1, 1), (1, 2), (1, 3)]
         todo = {}
 
-        def at(h, part, *calls):
-            todo.setdefault((h, part), []).extend(calls)
+        def at(s, *calls):
+            todo.setdefault(s, []).extend(calls)
 
         def later(fn, *args):
             return lambda: fn(*args)
 
-        def play(s, part):
-            for call in todo.pop((s, part), []):
+        def play(s):
+            for call in todo.pop(s, []):
                 call()
 
         SS = (False, False)
         SV = (False, True)
-        at(0, "W", later(copy_x, 0, 0, True), later(copy_x, 0, 1, True))
-        at(0, "X", later(copy_x, 1, 0, False))
-        at(1, "Q", later(quant_x, 0, 0), later(quant_x, 0, 1))
-        at(1, "X", later(copy_x, 1, 1, False))
-        at(2, "Q", later(quant_x, 1, 0), later(quant_x, 1, 1))
-        at(0, "X", later(load_k, 0))
+        U = [(0, 0), (1, 0), (0, 1), (1, 1), (0, 2), (0, 3), (1, 2), (1, 3)]
+        at("x0", later(copy_x, 0, 0), later(copy_x, 0, 1), later(copy_x, 1, 0))
+        at("x1", later(copy_x, 1, 1), later(load_k, 0))
+        at("q1", later(quant_x, 0, 0), later(quant_x, 0, 1))
+        at("q2", later(quant_x, 1, 0), later(quant_x, 1, 1))
         wj = [(0, 0), (1, 0), (0, 1), (1, 1), (2, 0), (3, 0), (2, 1), (3, 1)]
         for n in range(8):
             s = (1, 1, 2, 2, 3, 3, 4, 4)[n]
-            at(s, "X", later(transpose_w, *wj[n]), later(copy_w, *wj[n]))
-            at(s + 1, "Q", later(quant_w, *wj[n]))
-        at(1, "X", later(load_w, 1, 0), later(load_k, 1))
-        at(2, "X", later(load_w, 1, 1))
-        for n in range(4):
-            at(2, "X", later(dw_pair, 0, n, SS))
-        for n in range(2):
-            at(5, "X", later(dx_early, 0, n, (0, 1, 2)))
-        for n in range(4):
-            at(6, "X", later(dx_pair, 0, n, SS))
-        for n in range(4):
-            at(7, "X", later(dw_pair, 1, n, SS))
+            at(f"x{s}", later(transpose_w, *wj[n]), later(copy_w, *wj[n]))
+            at(f"q{s + 1}", later(quant_w, *wj[n]))
+            if n == 1:
+                at(f"x{s}", later(load_w, 1, 0), later(load_k, 1))
+            if n == 3:
+                at(f"x{s}", later(load_w, 1, 1))
+        at("x2", *[later(dw_pair, 0, n, SS) for n in range(4)])
+        at("x4", *[later(dw_pair, 1, n, SS) for n in range(4)])
+        at("x5", *[later(dx_part, 1, n, SS) for n in range(4)])
+        at("x6", *[later(dx_open, 0, n, (0, 1, 2)) for n in range(2)])
+        at("x7", *[later(dx_pair, 0, n, SS) for n in range(2)])
 
         for s in range(8):
-            for hh in range(2):
-                mult_a(U[s], hh)
-                mult_b(U[s], hh)
+            mult(U[s])
             if s >= 1:
-                adds(U[s - 1], 0, True)
-                adds(U[s - 1], 1, True)
-            play(s, "W")
-            if s >= 1:
-                adds(U[s - 1], 0, False)
-                adds(U[s - 1], 1, False)
+                add(U[s - 1], nc.gpsimd, 0, GPS_COLS)
+                add(U[s - 1], nc.vector, GPS_COLS, 512)
             if s >= 2:
                 quant_col(U[s - 2])
-            play(s, "Q")
+            play(f"q{s}")
             if s >= 1:
                 transpose_dz(U[s - 1])
                 copy_dz(U[s - 1])
                 quant_row(U[s - 1])
-            play(s, "X")
-        adds(U[7], 0, False, 0)
-        adds(U[7], 1, False, 0)
-        transpose_dz(U[7])
-        quant_row(U[7])
-        copy_dz(U[7], True)
+            play(f"x{s}")
+        SPOTS.extend([(ptab, "tab"), (ptab, "neg")])
+        add(U[7], nc.vector, 0, 512)
         quant_col(U[6])
+        dx_pair(0, 2, SV)
+        transpose_dz(U[7])
+        copy_dz(U[7], True)
+        quant_row(U[7])
         quant_col(U[7])
+        dx_pair(0, 3, SV)
         for m2 in range(4):
             dw_pair(2, m2, SV)
-        for t in range(4):
-            dx_pair(1, t, SV)
         for m2 in range(4):
-            dw_pair(3, m2, SV)
+            dw_pair(3, m2, SV if m2 < 2 else SS)
+        for t in range(4):
+            dx_pair(1, t, SS)

@@ -9,331 +9,397 @@ BF16 = mybir.dt.bfloat16
 I32 = mybir.dt.int32
 U32 = mybir.dt.uint32
 U8 = mybir.dt.uint8
-E4 = mybir.dt.float8_e4m3fn_x4
-E5 = mybir.dt.float8_e5m2_x4
+E4M3 = mybir.dt.float8_e4m3fn_x4
+E5M2 = mybir.dt.float8_e5m2_x4
 ALU = mybir.AluOpType
 ACT = mybir.ActivationFunctionType
 
 P = 128
-T, F, HD = 1024, 1024, 1024
+PACK = 4
+PASS = P * PACK
+HALF = 64
+RUN = 4
+HALVES = PASS // HALF
+POSITIONS = 256
+ROUNDS = POSITIONS // PACK
+TOKENS, IN_FEATURES, OUT_FEATURES = 1024, 1024, 1024
 THETA = 10000.0
-FLOPS = 2 * 2 * T * F * 2 * HD
-BYTES = 2 * (T * F + 2 * F * HD + 2 * T * HD) + 4 * (T * F + 2 * F * HD)
+FLOPS = 2 * 2 * TOKENS * IN_FEATURES * 2 * OUT_FEATURES
+BYTES = 2 * (TOKENS * IN_FEATURES + 2 * IN_FEATURES * OUT_FEATURES + 2 * TOKENS * OUT_FEATURES) + 4 * (
+    TOKENS * IN_FEATURES + 2 * IN_FEATURES * OUT_FEATURES
+)
 
-GPS_COLS = 448
+UNITS = ((0, 0), (1, 0), (0, 1), (1, 1), (0, 2), (1, 2), (0, 3), (1, 3))
+W_PIECES = ((0, 0), (1, 0), (0, 1), (1, 1), (2, 0), (3, 0), (2, 1), (3, 1))
+
+ORDER = (
+    "copy_x:0,1 copy_x:0,0",
+    "products:0 turn_w:0 copy_x:1,1",
+    "products:1 sum_vector:0,480 quantise_x:0,1 copy_w:0:sv quantise_x:0,0 sum_gpsimd:0,480 turn_dz:0 quantise_w:0 "
+    "copy_dz:0:ss quantise_by_token:0 sum_vector:1,480 copy_x:1,0",
+    "products:2 quantise_x:1,1 turn_w:1 copy_w:1:ss sum_gpsimd:1,480 quantise_w:1 turn_w:3 quantise_by_token:1 "
+    "copy_w:3:ss turn_dz:1 quantise_x:1,0 load_grad_1:1 copy_dz:1:ss load_grad_1:0",
+    "products:3 sum_vector:2,256 turn_w:2 copy_w:2:ss load_wk:0 sum_gpsimd:2,256 weight_gradient:0,0:ss "
+    "quantise_by_feature:0 quantise_by_token:2 turn_dz:2 quantise_by_feature:1",
+    "products:4 sum_vector:3,480 copy_dz:2:ss sum_gpsimd:3,480 load_wk:1 weight_gradient:0,3:ss turn_w:5 "
+    "quantise_by_feature:2 copy_w:5:ss weight_gradient:0,2:vs turn_w:4 copy_w:4:ss quantise_by_token:3 quantise_w:2 "
+    "weight_gradient:0,1:ss turn_dz:3 quantise_w:3 copy_dz:3:ss half_sum:0,0:ss turn_w:6 copy_w:6:ss",
+    "products:5 weight_gradient:1,2:ss sum_gpsimd:4,480 turn_w:7 quantise_by_feature:3 copy_w:7:ss sum_vector:4,480 "
+    "half_sum:0,1:ss quantise_by_token:4 turn_dz:4 half_sum:0,2:ss weight_gradient:1,3:ss",
+    "products:6 sum_vector:5,256 copy_dz:4:sv half_sum:0,3:ss sum_gpsimd:5,256 quantise_by_token:5 half_sum:1,3:ss "
+    "turn_dz:5 weight_gradient:1,1:ss weight_gradient:2,1:ss",
+    "products:7 half_sum:1,1:sv quantise_by_feature:4 sum_gpsimd:6,416 copy_dz:5:ss sum_vector:6,416 "
+    "weight_gradient:1,0:sv half_sum:1,2:sv turn_dz:6 quantise_by_token:6 quantise_w:5 sum_vector:7,0 copy_dz:6:ss "
+    "half_sum:1,0:ss weight_gradient:2,0:ss quantise_by_feature:5 quantise_by_token:7 weight_gradient:2,3:sv "
+    "turn_dz:7 quantise_w:6 weight_gradient:3,3:ss weight_gradient:3,0:ss quantise_by_feature:6 copy_dz:7:vs "
+    "weight_gradient:3,1:vv quantise_w:7 quantise_w:4 weight_gradient:2,2:ss quantise_by_feature:7 "
+    "weight_gradient:3,2:ss input_gradient:0,1 input_gradient:1,2 input_gradient:0,2 input_gradient:0,3 "
+    "input_gradient:1,3 input_gradient:1,0 input_gradient:1,1 input_gradient:0,0:halves",
+)
 
 
 def tile_selfattention_pa_v_kernel(tc, x, wq, bq, wk, bk, grad_0, grad_1, out_0, out_1, out_2):
     nc = tc.nc
-    xf = x.rearrange("b s f -> (b s) f").rearrange("(g p j) f -> g p j f", p=P, j=4)
-    gf = [a.rearrange("b s h d -> (b s) (h d)").rearrange("(g p j) c -> g p j c", p=P, j=4) for a in (grad_0, grad_1)]
-    wf = [a.rearrange("f h d -> f (h d)").rearrange("(z a p) c -> z p a c", z=2, p=P) for a in (wq, wk)]
-    o0 = out_0.rearrange("b s f -> (b s) f").rearrange("(g p j) f -> g j p f", p=P, j=4)
-    ow = [a.rearrange("f h d -> f (h d)").rearrange("(m p) c -> m p c", p=P) for a in (out_1, out_2)]
+    x_rows = x.rearrange("b s f -> (b s) f").rearrange("(g p t) f -> g p t f", p=P, t=PACK)
+    grad_rows = [
+        grad.rearrange("b s h d -> (b s) (h d)").rearrange("(g p t) c -> g p t c", p=P, t=PACK)
+        for grad in (grad_0, grad_1)
+    ]
+    w_rows = [w.rearrange("f h d -> f (h d)").rearrange("(z a p) c -> z p a c", z=2, p=P) for w in (wq, wk)]
+    out_0_rows = out_0.rearrange("b s f -> (b s) f").rearrange("(g p t) (z f) -> g t p z f", p=P, t=PACK, z=2)
+    dw_rows = [
+        out.rearrange("f h d -> f (h d)").rearrange("(m a p) (k c) -> m k p a c", a=2, p=P, k=2) for out in (out_1, out_2)
+    ]
 
     with ExitStack() as ctx:
         const = ctx.enter_context(tc.tile_pool(name="const", bufs=1))
-        inp = ctx.enter_context(tc.tile_pool(name="inp", bufs=1))
-        keep = ctx.enter_context(tc.tile_pool(name="keep", bufs=1))
+        inputs = ctx.enter_context(tc.tile_pool(name="inputs", bufs=1))
+        operands = ctx.enter_context(tc.tile_pool(name="operands", bufs=1))
         work = ctx.enter_context(tc.tile_pool(name="work", bufs=2))
-        outs = ctx.enter_context(tc.tile_pool(name="outs", bufs=6))
-        ptab = ctx.enter_context(tc.psum_pool(name="ptab", bufs=1))
-        ptr = ctx.enter_context(tc.psum_pool(name="ptr", bufs=2))
-        pmm = ctx.enter_context(tc.psum_pool(name="pmm", bufs=4))
+        results = ctx.enter_context(tc.tile_pool(name="results", bufs=6))
+        table_banks = ctx.enter_context(tc.psum_pool(name="table_banks", bufs=1))
+        turn_banks = ctx.enter_context(tc.psum_pool(name="turn_banks", bufs=2))
+        sum_banks = ctx.enter_context(tc.psum_pool(name="sum_banks", bufs=4))
         ctx.enter_context(tc.manual_schedule())
 
-        gt, xt, wt = {}, {}, {}
+        grad_tile, x_tile, w_tile = {}, {}, {}
 
-        def load_q(g, k):
-            t = inp.tile([P, 4, 512], BF16, name=f"gq{g}{k}", align_bytes=64)
-            nc.sync.dma_start(out=t[:], in_=gf[0][g][:, :, 512 * k : 512 * k + 512])
-            gt[g, k] = t
+        def load_grad_0(g, k):
+            tile = inputs.tile([P, PACK, PASS], BF16, name=f"grad_{g}{k}", align_bytes=64)
+            nc.sync.dma_start(out=tile[:], in_=grad_rows[0][g][:, :, PASS * k : PASS * (k + 1)])
+            grad_tile[g, k] = tile
 
-        def load_k(g):
-            t = inp.tile([P, 4, 1024], BF16, name=f"xg{g}", align_bytes=64)
-            nc.sync.dma_start(out=t[:], in_=gf[1][g])
-            gt[g, 2] = t[:, :, 0:512]
-            gt[g, 3] = t[:, :, 512:1024]
+        def load_grad_1(g):
+            for k in (2, 3):
+                tile = inputs.tile([P, PACK, PASS], BF16, name=f"x_{g}{k - 2}", align_bytes=64)
+                nc.sync.dma_start(out=tile[:], in_=grad_rows[1][g][:, :, PASS * (k - 2) : PASS * (k - 1)])
+                grad_tile[g, k] = tile
 
-        def load_x(g):
-            t = inp.tile([P, 4, 1024], BF16, name=f"xg{g}", align_bytes=64)
-            nc.sync.dma_start(out=t[:], in_=xf[g])
-            xt[g] = t
+        def load_x(g, z):
+            tile = inputs.tile([P, PACK, PASS], BF16, name=f"x_{g}{z}", align_bytes=64)
+            nc.sync.dma_start(out=tile[:], in_=x_rows[g][:, :, PASS * z : PASS * (z + 1)])
+            x_tile[g, z] = tile
 
-        def load_w(l, z):
-            t = inp.tile([P, 4, 1024], BF16, name=f"w{z}", align_bytes=64)
-            nc.sync.dma_start(out=t[:], in_=wf[l][z])
-            wt[l, z] = t
+        def load_w(layer, z):
+            tile = inputs.tile([P, PACK, OUT_FEATURES], BF16, name=f"w_{z}", align_bytes=64)
+            nc.sync.dma_start(out=tile[:], in_=w_rows[layer][z])
+            w_tile[layer, z] = tile
 
-        load_q(0, 0)
-        load_x(0)
-        load_q(1, 0)
-        load_x(1)
-        load_q(0, 1)
+        def load_wk(z):
+            load_w(1, z)
+
+        load_x(0, 0)
+        load_grad_0(0, 0)
+        load_x(0, 1)
+        load_grad_0(1, 0)
+        load_x(1, 0)
+        load_x(1, 1)
+        load_grad_0(0, 1)
         load_w(0, 0)
         load_w(0, 1)
-        load_q(1, 1)
+        load_grad_0(1, 1)
 
-        qi = const.tile([P, 1], I32)
-        nc.gpsimd.iota(qi[:], pattern=[[0, 1]], base=0, channel_multiplier=1)
-        pos = const.tile([P, 256], F32)
-        nc.gpsimd.iota(pos[:], pattern=[[1, 4], [4, 64]], base=0, channel_multiplier=0, allow_small_or_imprecise_dtypes=True)
-        ident = const.tile([P, P], F32)
-        make_identity(nc, ident[:])
+        row_number = const.tile([P, 1], I32)
+        nc.gpsimd.iota(row_number[:], pattern=[[0, 1]], base=0, channel_multiplier=1)
+        position = const.tile([P, POSITIONS], F32)
+        nc.gpsimd.iota(
+            position[:],
+            pattern=[[1, PACK], [PACK, ROUNDS]],
+            base=0,
+            channel_multiplier=0,
+            allow_small_or_imprecise_dtypes=True,
+        )
+        identity = const.tile([P, P], F32)
+        make_identity(nc, identity[:])
         bits = const.tile([P, 7], I32)
         for b in range(7):
-            nc.vector.tensor_scalar(out=bits[:, b : b + 1], in0=qi[:], scalar1=b, scalar2=1, op0=ALU.logical_shift_right, op1=ALU.bitwise_and)
-        fac = const.tile([P, 6], F32)
-        for b in range(6):
-            r = THETA ** (-(2.0**b) / 64.0)
-            nc.vector.tensor_scalar(out=fac[:, b : b + 1], in0=bits[:, b : b + 1], scalar1=r - 1.0, scalar2=1.0, op0=ALU.mult, op1=ALU.add)
-        phase = const.tile([P, 1], F32)
-        nc.vector.tensor_scalar(out=phase[:], in0=bits[:, 6:7], scalar1=-0.25, scalar2=0.25, op0=ALU.mult, op1=ALU.add)
-        fac3 = const.tile([P, 3], F32)
-        nc.vector.tensor_tensor(out=fac3[:], in0=fac[:, 0:3], in1=fac[:, 3:6], op=ALU.mult)
-        fac2 = const.tile([P, 1], F32)
-        nc.vector.tensor_tensor(out=fac2[:], in0=fac3[:, 0:1], in1=fac3[:, 1:2], op=ALU.mult)
-        freq = const.tile([P, 1], F32)
-        nc.vector.scalar_tensor_tensor(out=freq[:], in0=fac2[:], scalar=0.5 / math.pi, in1=fac3[:, 2:3], op0=ALU.mult, op1=ALU.mult)
-        turns = const.tile([P, 256], F32)
-        nc.vector.tensor_scalar(out=turns[:], in0=pos[:], scalar1=freq[:], scalar2=phase[:], op0=ALU.mult, op1=ALU.add)
-        whole = const.tile([P, 256], I32)
-        nc.vector.tensor_copy(out=whole[:], in_=turns[:])
-        rest = const.tile([P, 4, 64], F32)
-        nc.vector.tensor_tensor(out=rest[:].rearrange("p t s -> p (t s)"), in0=turns[:], in1=whole[:], op=ALU.subtract)
-        tabs = []
-        for sign in (1.0, -1.0):
-            wave = const.tile([P, 4, 2, 64], F32, name="wave", bufs=2)
-            nc.scalar.activation(out=wave[:], in_=rest[:].unsqueeze(2).to_broadcast([P, 4, 2, 64]), func=ACT.Sin, scale=sign * 2.0 * math.pi)
-            tab = ptab.tile([P, 4, P], F32, name="tab" if sign > 0 else "neg")
-            for t in range(4):
-                nc.tensor.transpose(tab[:, t, :], wave[:, t, :, :].rearrange("p a s -> p (a s)"), ident[:])
-            tabs.append(tab)
-        cos = tabs[0][:, :, 0:64].unsqueeze(2)
-        sin = tabs[0][:, :, 64:128].unsqueeze(2)
-        nsin = tabs[1][:, :, 64:128].unsqueeze(2)
-
-        AB, DZ, ROW, DZT, COL = {}, {}, {}, {}, {}
-        banks = {}
-
-        def mult(u):
-            src = gt[u][:].rearrange("p t (q j) -> p t q j", j=64)
-            a = work.tile([P, 4, 8, 64], F32, name="prod_a", align_bytes=64)
-            nc.vector.tensor_tensor(out=a[:], in0=src, in1=cos.to_broadcast([P, 4, 8, 64]), op=ALU.mult)
-            b = work.tile([P, 4, 8, 64], F32, name="prod_b", align_bytes=64)
-            nc.vector.tensor_tensor(out=b[:, :, 0:8:2, :], in0=src[:, :, 1:8:2, :], in1=sin.to_broadcast([P, 4, 4, 64]), op=ALU.mult)
-            nc.vector.tensor_tensor(out=b[:, :, 1:8:2, :], in0=src[:, :, 0:8:2, :], in1=nsin.to_broadcast([P, 4, 4, 64]), op=ALU.mult)
-            AB[u] = (a, b)
-
-        def add(u, eng, lo, hi):
-            if u not in DZ:
-                dz = work.tile([P, 512, 4], BF16, name="dz", bufs=1, align_bytes=64)
-                DZ[u] = dz
-            a, b = [s[:].rearrange("p t q j -> p t (q j)")[:, :, lo:hi].rearrange("p t (c i) -> p c t i", i=4) for s in AB[u]]
-            eng.tensor_tensor(out=DZ[u][:, lo:hi, :].rearrange("p (c i) t -> p c t i", i=4), in0=a, in1=b, op=ALU.add)
-
-        def quant(dst, src, fmt, key, name):
-            codes = keep.tile([P, 512], U32, name=f"{name}c", align_bytes=64)
-            scales = keep.tile([P, 512], U8, name=f"{name}s", align_bytes=64)
-            nc.vector.quantize_mx(out=codes[:].bitcast(fmt), scales=scales[:], in_=src[:].rearrange("p c t -> p (c t)"))
-            dst[key] = (codes, scales)
-
-        def quant_row(u):
-            quant(ROW, DZ[u], E5, u, f"r{u[0]}{u[1]}")
-
-        def transpose_dz(u):
-            words = DZ[u][:].rearrange("p c t -> p (c t)").bitcast(F32)
-            for tp in range(2):
-                bank = ptr.tile([P, 4, P], F32, name="tr")
-                for t in range(4):
-                    nc.tensor.transpose(bank[:, t, :], words[:, 2 * t + tp : 1024 : 8], ident[:])
-                banks[u, tp] = bank
-
-        def copy_dz(u, vec=False):
-            dzt = work.tile([P, 512, 4], BF16, name="dzt", bufs=2, align_bytes=64)
-            for tp in range(2):
-                copy = nc.vector.tensor_copy if vec and tp == 1 else nc.scalar.copy
-                copy(
-                    out=dzt[:, 256 * tp : 256 * tp + 256, :].rearrange("i (e p) t -> i e p t", e=2),
-                    in_=banks[u, tp][:].rearrange("i t p -> i (t p)").bitcast(BF16).rearrange("i (t p e) -> i e p t", t=4, e=2),
-                )
-            DZT[u] = dzt
-
-        def quant_col(u):
-            quant(COL, DZT[u], E5, u, f"c{u[0]}{u[1]}")
-
-        XI, XQ = {}, {}
-
-        def copy_x(g, h):
-            xi = work.tile([P, 512, 4], BF16, name="stage", bufs=4, align_bytes=64)
-            nc.scalar.copy(
-                out=xi[:].rearrange("p (c i) t -> p c t i", i=4),
-                in_=xt[g][:, :, 512 * h : 512 * h + 512].rearrange("p t (c i) -> p c t i", i=4),
+            nc.vector.tensor_scalar(
+                out=bits[:, b : b + 1],
+                in0=row_number[:],
+                scalar1=b,
+                scalar2=1,
+                op0=ALU.logical_shift_right,
+                op1=ALU.bitwise_and,
             )
-            XI[g, h] = xi
+        factors = const.tile([P, 6], F32)
+        for b in range(6):
+            nc.vector.tensor_scalar(
+                out=factors[:, b : b + 1],
+                in0=bits[:, b : b + 1],
+                scalar1=THETA ** (-(2.0**b) / HALF) - 1.0,
+                scalar2=1.0,
+                op0=ALU.mult,
+                op1=ALU.add,
+            )
+        phase = const.tile([P, 1], F32)
+        nc.vector.tensor_scalar(
+            out=phase[:], in0=bits[:, 6:7], scalar1=-0.25, scalar2=0.25, op0=ALU.mult, op1=ALU.add
+        )
+        triples = const.tile([P, 3], F32)
+        nc.vector.tensor_tensor(out=triples[:], in0=factors[:, 0:3], in1=factors[:, 3:6], op=ALU.mult)
+        pair = const.tile([P, 1], F32)
+        nc.vector.tensor_tensor(out=pair[:], in0=triples[:, 0:1], in1=triples[:, 1:2], op=ALU.mult)
+        turns_per_step = const.tile([P, 1], F32)
+        nc.vector.scalar_tensor_tensor(
+            out=turns_per_step[:],
+            in0=pair[:],
+            scalar=0.5 / math.pi,
+            in1=triples[:, 2:3],
+            op0=ALU.mult,
+            op1=ALU.mult,
+        )
+        turns = const.tile([P, POSITIONS], F32)
+        nc.vector.tensor_scalar(
+            out=turns[:], in0=position[:], scalar1=turns_per_step[:], scalar2=phase[:], op0=ALU.mult, op1=ALU.add
+        )
+        whole_turns = const.tile([P, POSITIONS], I32)
+        nc.vector.tensor_copy(out=whole_turns[:], in_=turns[:])
+        rest = const.tile([P, PACK, ROUNDS], F32)
+        nc.vector.tensor_tensor(
+            out=rest[:].rearrange("q t s -> q (t s)"), in0=turns[:], in1=whole_turns[:], op=ALU.subtract
+        )
+        tables = []
+        for sign in (1.0, -1.0):
+            wave = const.tile([P, PACK, 2, ROUNDS], F32, name="wave", bufs=2)
+            nc.scalar.activation(
+                out=wave[:],
+                in_=rest[:].unsqueeze(2).to_broadcast([P, PACK, 2, ROUNDS]),
+                func=ACT.Sin,
+                scale=sign * 2.0 * math.pi,
+            )
+            table = table_banks.tile([P, PACK, P], F32, name="table" if sign > 0 else "negative_table")
+            for t in range(PACK):
+                nc.tensor.transpose(table[:, t, :], wave[:, t, :, :].rearrange("q a s -> q (a s)"), identity[:])
+            tables.append(table)
+        cosine = tables[0][:, :, 0:HALF].unsqueeze(2)
+        sine = tables[0][:, :, HALF:P].unsqueeze(2)
+        minus_sine = tables[1][:, :, HALF:P].unsqueeze(2)
 
-        def quant_x(g, h):
-            quant(XQ, XI[g, h], E4, (g, h), f"x{g}{h}")
+        product_tiles, dz = {}, {}
 
-        WT, WQ = {}, {}
-
-        def transpose_w(k, z):
-            words = wt[k // 2, z][:].rearrange("p a c -> p (a c)").bitcast(F32)
-            for y in range(2):
-                bank = ptr.tile([P, 2, 2, P], F32, name="tr")
-                for a in range(2):
-                    for u in range(2):
-                        s = 512 * (2 * y + a) + 256 * (k % 2)
-                        nc.tensor.transpose(bank[:, a, u, :], words[:, s + u : s + 256 : 2], ident[:])
-                banks["w", k, z, y] = bank
-
-        def copy_w(k, z):
-            wtt = work.tile([P, 512, 4], BF16, name="stage", bufs=4, align_bytes=64)
-            wwords = wtt[:].rearrange("p c t -> p (c t)").bitcast(F32)
-            for y in range(2):
-                nc.scalar.copy(
-                    out=wwords[:, 512 * y : 512 * y + 512].rearrange("i (a r u) -> i a r u", a=2, u=2),
-                    in_=banks["w", k, z, y][:].rearrange("i a u r -> i a r u"),
+        def products(u):
+            grad = grad_tile[UNITS[u]][:].rearrange("p t (q j) -> p t q j", j=HALF)
+            straight = work.tile([P, PACK, HALVES, HALF], F32, name="straight", align_bytes=64)
+            nc.vector.tensor_tensor(
+                out=straight[:], in0=grad, in1=cosine.to_broadcast([P, PACK, HALVES, HALF]), op=ALU.mult
+            )
+            crossed = work.tile([P, PACK, HALVES, HALF], F32, name="crossed", align_bytes=64)
+            for to_half, table in ((0, sine), (1, minus_sine)):
+                nc.vector.tensor_tensor(
+                    out=crossed[:, :, to_half:HALVES:2, :],
+                    in0=grad[:, :, 1 - to_half : HALVES : 2, :],
+                    in1=table.to_broadcast([P, PACK, HALVES // 2, HALF]),
+                    op=ALU.mult,
                 )
-            WT[k, z] = wtt
+            product_tiles[u] = (straight, crossed)
+            if u == len(UNITS) - 1:
+                bank_cycle.extend(
+                    [(sum_banks, "sum"), (table_banks, "table"), (sum_banks, "sum"), (table_banks, "negative_table")]
+                )
 
-        def quant_w(k, z):
-            quant(WQ, WT[k, z], E4, (k, z), f"w{k}{z}")
+        def sum_columns(u, engine, first, last):
+            if u not in dz:
+                tile = work.tile([P, PASS, PACK], BF16, name="dz", bufs=1, align_bytes=64)
+                dz[u] = tile
+            terms = [
+                tile[:].rearrange("p t q j -> p t (q j)")[:, :, first:last].rearrange("p t (c r) -> p c t r", r=RUN)
+                for tile in product_tiles[u]
+            ]
+            engine.tensor_tensor(
+                out=dz[u][:, first:last, :].rearrange("p (c r) t -> p c t r", r=RUN),
+                in0=terms[0],
+                in1=terms[1],
+                op=ALU.add,
+            )
 
-        def mx(bank, lhs, lcol, lfmt, rhs, rfmt, start, stop):
+        def sum_gpsimd(u, columns):
+            sum_columns(u, nc.gpsimd, 0, columns)
+
+        def sum_vector(u, columns):
+            sum_columns(u, nc.vector, columns, PASS)
+
+        dz_by_token, dz_by_feature, x_by_token, w_by_feature = {}, {}, {}, {}
+
+        def quantise(tile, fmt, name):
+            codes = operands.tile([P, PASS], U32, name=f"{name}_codes", align_bytes=64)
+            scales = operands.tile([P, PASS], U8, name=f"{name}_scales", align_bytes=64)
+            nc.vector.quantize_mx(
+                out=codes[:].bitcast(fmt), scales=scales[:], in_=tile[:].rearrange("p c i -> p (c i)")
+            )
+            return codes, scales
+
+        def move(engine, out, in_):
+            copy = nc.vector.tensor_copy if engine == "v" else nc.scalar.copy
+            copy(out=out, in_=in_)
+
+        def quantise_by_token(u):
+            g, k = UNITS[u]
+            dz_by_token[g, k] = quantise(dz[u], E5M2, f"dz_by_token_{g}{k}")
+
+        turned, dz_turned = {}, {}
+
+        def turn_dz(u):
+            words = dz[u][:].rearrange("p c t -> p (c t)").bitcast(F32)
+            for h in range(2):
+                bank = turn_banks.tile([P, PACK, P], F32, name="turn")
+                for i in range(PACK):
+                    nc.tensor.transpose(bank[:, i, :], words[:, 2 * i + h : 2 * PASS : 2 * PACK], identity[:])
+                turned[u, h] = bank
+
+        def copy_dz(u, engines):
+            tile = work.tile([P, PASS, PACK], BF16, name="dz_turned", align_bytes=64)
+            for h in range(2):
+                move(
+                    engines[h],
+                    tile[:, 2 * P * h : 2 * P * (h + 1), :].rearrange("p (e n) i -> p e n i", e=2),
+                    turned[u, h][:]
+                    .rearrange("p i n -> p (i n)")
+                    .bitcast(BF16)
+                    .rearrange("p (i n e) -> p e n i", i=PACK, e=2),
+                )
+            dz_turned[u] = tile
+
+        def quantise_by_feature(u):
+            g, k = UNITS[u]
+            dz_by_feature[g, k] = quantise(dz_turned[u], E5M2, f"dz_by_feature_{g}{k % 2}")
+
+        x_laid, w_laid = {}, {}
+
+        def copy_x(g, z):
+            tile = work.tile([P, PASS, PACK], BF16, name="laid", bufs=4, align_bytes=64)
+            nc.scalar.copy(
+                out=tile[:].rearrange("p (c r) t -> p c t r", r=RUN),
+                in_=x_tile[g, z][:].rearrange("p t (c r) -> p c t r", r=RUN),
+            )
+            x_laid[g, z] = tile
+
+        def quantise_x(g, z):
+            x_by_token[g, z] = quantise(x_laid[g, z], E4M3, f"x_by_token_{g}{z}")
+
+        def turn_w(n):
+            k, z = W_PIECES[n]
+            words = w_tile[k // 2, z][:].rearrange("p a c -> p (a c)").bitcast(F32)
+            for y in range(2):
+                bank = turn_banks.tile([P, 2, 2, P], F32, name="turn")
+                for a in range(2):
+                    first = OUT_FEATURES // 2 * (2 * y + a) + PASS // 2 * (k % 2)
+                    for u in range(2):
+                        nc.tensor.transpose(bank[:, a, u, :], words[:, first + u : first + PASS // 2 : 2], identity[:])
+                turned["w", n, y] = bank
+
+        def copy_w(n, engines):
+            tile = work.tile([P, PASS, PACK], BF16, name="laid", bufs=4, align_bytes=64)
+            words = tile[:].rearrange("p c i -> p (c i)").bitcast(F32)
+            for y in range(2):
+                move(
+                    engines[y],
+                    words[:, PASS * y : PASS * (y + 1)].rearrange("p (a f u) -> p a f u", a=2, u=2),
+                    turned["w", n, y][:].rearrange("p a u f -> p a f u"),
+                )
+            w_laid[n] = tile
+
+        def quantise_w(n):
+            k, z = W_PIECES[n]
+            w_by_feature[k, z] = quantise(w_laid[n], E4M3, f"w_by_feature_{k}{z}")
+
+        bank_cycle = [(sum_banks, "sum")]
+        banks_taken = [0]
+
+        def new_bank():
+            pool, name = bank_cycle[banks_taken[0] % len(bank_cycle)]
+            banks_taken[0] += 1
+            bank = pool.tile([P, PASS], F32, name=name)
+            return bank
+
+        def multiply(bank, stationary, column, stationary_fmt, moving, moving_fmt, start, stop):
             nc.tensor.matmul_mx(
                 out=bank[:],
-                lhsT=lhs[0][:, lcol : lcol + P].bitcast(lfmt),
-                lhsT_scale=lhs[1][:, lcol : lcol + P],
-                rhs=rhs[0][:].bitcast(rfmt),
-                rhs_scale=rhs[1][:],
+                lhsT=stationary[0][:, column : column + P].bitcast(stationary_fmt),
+                lhsT_scale=stationary[1][:, column : column + P],
+                rhs=moving[0][:].bitcast(moving_fmt),
+                rhs_scale=moving[1][:],
                 start=start,
                 stop=stop,
             )
 
-        def evac(dst, bank, vec):
-            if vec:
-                nc.vector.tensor_copy(out=dst, in_=bank[:])
-            else:
-                nc.scalar.copy(out=dst, in_=bank[:])
+        def weight_gradient(k, m, engines):
+            result = results.tile([P, 2, PASS], F32, name="result")
+            for a in range(2):
+                bank = new_bank()
+                f = P * (2 * m + a)
+                for g in range(2):
+                    multiply(bank, x_by_token[g, f // PASS], f % PASS, E4M3, dz_by_token[g, k], E5M2, g == 0, g == 1)
+                move(engines[a], result[:, a, :], bank[:])
+            nc.sync.dma_start(out=dw_rows[k // 2][m][k % 2], in_=result[:])
 
-        SPOTS = [(pmm, "mm")]
-        turn = [0]
+        half_sums = {}
 
-        def new_bank():
-            pool, name = SPOTS[turn[0] % len(SPOTS)]
-            turn[0] += 1
-            bank = pool.tile([P, 512], F32, name=name)
+        def dx_sum(g, t, z, blocks):
+            bank = new_bank()
+            for k in blocks:
+                multiply(
+                    bank, dz_by_feature[g, k], P * t, E5M2, w_by_feature[k, z], E4M3, k == blocks[0], k == blocks[-1]
+                )
             return bank
 
-        def dw_pair(k, m2, vecs):
-            ot = outs.tile([P, 2, 512], F32, name="ot")
-            for a in range(2):
-                m = 2 * m2 + a
-                bank = new_bank()
-                for g in range(2):
-                    mx(bank, XQ[g, m // 4], 128 * (m % 4), E4, ROW[g, k], E5, g == 0, g == 1)
-                evac(ot[:, a, :], bank, vecs[a])
-            nc.sync.dma_start(
-                out=ow[k // 2][2 * m2 : 2 * m2 + 2, :, 512 * (k % 2) : 512 * (k % 2) + 512].rearrange("a p c -> p a c"),
-                in_=ot[:],
-            )
-
-        OPEN, PART = {}, {}
-
-        def dx_pass(bank, g, t, z, ks, first, last):
-            for k in ks:
-                mx(bank, COL[g, k], 128 * t, E5, WQ[k, z], E4, k == first, k == last)
-
-        def dx_open(g, t, ks):
+        def half_sum(g, t, engines):
+            kept = results.tile([P, 2, PASS], F32, name=f"half_sum_{g}{t}", bufs=1)
             for z in range(2):
-                bank = new_bank()
-                OPEN[g, t, z] = bank
-                dx_pass(bank, g, t, z, ks, ks[0], 3)
+                bank = dx_sum(g, t, z, (0, 1))
+                move(engines[z], kept[:, z, :], bank[:])
+            half_sums[g, t] = kept
 
-        def dx_part(g, t, vecs):
-            part = outs.tile([P, 2, 512], F32, name=f"part{g}{t}", bufs=1)
+        def input_gradient(g, t, stores="whole"):
+            result = results.tile([P, 2, PASS], F32, name="result")
             for z in range(2):
-                bank = new_bank()
-                dx_pass(bank, g, t, z, (0, 1), 0, 1)
-                evac(part[:, z, :], bank, vecs[z])
-            PART[g, t] = part
+                bank = dx_sum(g, t, z, (2, 3))
+                nc.vector.tensor_tensor(out=result[:, z, :], in0=bank[:], in1=half_sums[g, t][:, z, :], op=ALU.add)
+            if stores == "halves":
+                for z in range(2):
+                    nc.sync.dma_start(out=out_0_rows[g][t][:, z, :], in_=result[:, z, :])
+            else:
+                nc.sync.dma_start(out=out_0_rows[g][t], in_=result[:])
 
-        def dx_pair(g, t, vecs):
-            ot = outs.tile([P, 2, 512], F32, name="ot")
-            part = PART.get((g, t))
-            for z in range(2):
-                if (g, t, z) in OPEN:
-                    bank = OPEN[g, t, z]
-                    dx_pass(bank, g, t, z, (3,), -1, 3)
-                else:
-                    bank = new_bank()
-                    dx_pass(bank, g, t, z, (2, 3) if part is not None else (0, 1, 2, 3), 2 if part is not None else 0, 3)
-                if part is not None:
-                    nc.vector.tensor_tensor(out=ot[:, z, :], in0=bank[:], in1=part[:, z, :], op=ALU.add)
-                else:
-                    evac(ot[:, z, :], bank, vecs[z])
-            nc.sync.dma_start(out=o0[g][t], in_=ot[:].rearrange("p z f -> p (z f)"))
-
-        todo = {}
-
-        def at(s, *calls):
-            todo.setdefault(s, []).extend(calls)
-
-        def later(fn, *args):
-            return lambda: fn(*args)
-
-        def play(s):
-            for call in todo.pop(s, []):
-                call()
-
-        SS = (False, False)
-        SV = (False, True)
-        U = [(0, 0), (1, 0), (0, 1), (1, 1), (0, 2), (0, 3), (1, 2), (1, 3)]
-        at("x0", later(copy_x, 0, 0), later(copy_x, 0, 1), later(copy_x, 1, 0))
-        at("x1", later(copy_x, 1, 1), later(load_k, 0))
-        at("q1", later(quant_x, 0, 0), later(quant_x, 0, 1))
-        at("q2", later(quant_x, 1, 0), later(quant_x, 1, 1))
-        wj = [(0, 0), (1, 0), (0, 1), (1, 1), (2, 0), (3, 0), (2, 1), (3, 1)]
-        for n in range(8):
-            s = (1, 1, 2, 2, 3, 3, 4, 4)[n]
-            at(f"x{s}", later(transpose_w, *wj[n]), later(copy_w, *wj[n]))
-            at(f"q{s + 1}", later(quant_w, *wj[n]))
-            if n == 1:
-                at(f"x{s}", later(load_w, 1, 0), later(load_k, 1))
-            if n == 3:
-                at(f"x{s}", later(load_w, 1, 1))
-        at("x2", *[later(dw_pair, 0, n, SS) for n in range(4)])
-        at("x4", *[later(dw_pair, 1, n, SS) for n in range(4)])
-        at("x5", *[later(dx_part, 1, n, SS) for n in range(4)])
-        at("x6", *[later(dx_open, 0, n, (0, 1, 2)) for n in range(2)])
-        at("x7", *[later(dx_pair, 0, n, SS) for n in range(2)])
-
-        for s in range(8):
-            mult(U[s])
-            if s >= 1:
-                add(U[s - 1], nc.gpsimd, 0, GPS_COLS)
-                add(U[s - 1], nc.vector, GPS_COLS, 512)
-            if s >= 2:
-                quant_col(U[s - 2])
-            play(f"q{s}")
-            if s >= 1:
-                transpose_dz(U[s - 1])
-                copy_dz(U[s - 1])
-                quant_row(U[s - 1])
-            play(f"x{s}")
-        SPOTS.extend([(ptab, "tab"), (ptab, "neg")])
-        add(U[7], nc.vector, 0, 512)
-        quant_col(U[6])
-        dx_pair(0, 2, SV)
-        transpose_dz(U[7])
-        copy_dz(U[7], True)
-        quant_row(U[7])
-        quant_col(U[7])
-        dx_pair(0, 3, SV)
-        for m2 in range(4):
-            dw_pair(2, m2, SV)
-        for m2 in range(4):
-            dw_pair(3, m2, SV if m2 < 2 else SS)
-        for t in range(4):
-            dx_pair(1, t, SS)
+        steps = {
+            "load_grad_1": load_grad_1,
+            "load_wk": load_wk,
+            "products": products,
+            "sum_gpsimd": sum_gpsimd,
+            "sum_vector": sum_vector,
+            "turn_dz": turn_dz,
+            "copy_dz": copy_dz,
+            "quantise_by_token": quantise_by_token,
+            "quantise_by_feature": quantise_by_feature,
+            "copy_x": copy_x,
+            "quantise_x": quantise_x,
+            "turn_w": turn_w,
+            "copy_w": copy_w,
+            "quantise_w": quantise_w,
+            "weight_gradient": weight_gradient,
+            "half_sum": half_sum,
+            "input_gradient": input_gradient,
+        }
+        for line in ORDER:
+            for step in line.split():
+                parts = step.split(":")
+                steps[parts[0]](*[int(number) for number in parts[1].split(",")], *parts[2:])

import math
from contextlib import ExitStack

import concourse.mybir as mybir
from concourse.masks import make_identity

F32 = mybir.dt.float32
BF16 = mybir.dt.bfloat16
I32 = mybir.dt.int32
U32 = mybir.dt.uint32
U8 = mybir.dt.uint8
E4M3 = mybir.dt.float8_e4m3fn_x4
E5M2 = mybir.dt.float8_e5m2_x4
ALU = mybir.AluOpType
ACT = mybir.ActivationFunctionType

P = 128
PACK = 4
PASS = P * PACK
HALF = 64
RUN = 4
HALVES = PASS // HALF
POSITIONS = 256
ROUNDS = POSITIONS // PACK
TOKENS, IN_FEATURES, OUT_FEATURES = 1024, 1024, 1024
THETA = 10000.0
FLOPS = 2 * 2 * TOKENS * IN_FEATURES * 2 * OUT_FEATURES
BYTES = 2 * (TOKENS * IN_FEATURES + 2 * IN_FEATURES * OUT_FEATURES + 2 * TOKENS * OUT_FEATURES) + 4 * (
    TOKENS * IN_FEATURES + 2 * IN_FEATURES * OUT_FEATURES
)

UNITS = ((0, 0), (1, 0), (0, 1), (1, 1), (0, 2), (1, 2), (0, 3), (1, 3))
W_PIECES = ((0, 0), (1, 0), (0, 1), (1, 1), (2, 0), (3, 0), (2, 1), (3, 1))

ORDER = (
    "copy_x:0,1 copy_x:0,0",
    "products:0 turn_w:0 copy_x:1,1",
    "products:1 sum_vector:0,480 quantise_x:0,1 copy_w:0:sv quantise_x:0,0 sum_gpsimd:0,480 turn_dz:0 quantise_w:0 "
    "copy_dz:0:ss quantise_by_token:0 sum_vector:1,480 copy_x:1,0",
    "products:2 quantise_x:1,1 turn_w:1 copy_w:1:ss sum_gpsimd:1,480 quantise_w:1 turn_w:3 quantise_by_token:1 "
    "copy_w:3:ss turn_dz:1 quantise_x:1,0 load_grad_1:1 copy_dz:1:ss load_grad_1:0",
    "products:3 sum_vector:2,256 turn_w:2 copy_w:2:ss load_wk:0 sum_gpsimd:2,256 weight_gradient:0,0:ss "
    "quantise_by_feature:0 quantise_by_token:2 turn_dz:2 quantise_by_feature:1",
    "products:4 sum_vector:3,480 copy_dz:2:ss sum_gpsimd:3,480 load_wk:1 weight_gradient:0,3:ss turn_w:5 "
    "quantise_by_feature:2 copy_w:5:ss weight_gradient:0,2:vs turn_w:4 copy_w:4:ss quantise_by_token:3 quantise_w:2 "
    "weight_gradient:0,1:ss turn_dz:3 quantise_w:3 copy_dz:3:ss half_sum:0,0:ss turn_w:6 copy_w:6:ss",
    "products:5 weight_gradient:1,2:ss sum_gpsimd:4,480 turn_w:7 quantise_by_feature:3 copy_w:7:ss sum_vector:4,480 "
    "half_sum:0,1:ss quantise_by_token:4 turn_dz:4 half_sum:0,2:ss weight_gradient:1,3:ss",
    "products:6 sum_vector:5,256 copy_dz:4:sv half_sum:0,3:ss sum_gpsimd:5,256 quantise_by_token:5 half_sum:1,3:ss "
    "turn_dz:5 weight_gradient:1,1:ss weight_gradient:2,1:ss",
    "products:7 half_sum:1,1:sv quantise_by_feature:4 sum_gpsimd:6,416 copy_dz:5:ss sum_vector:6,416 "
    "weight_gradient:1,0:sv half_sum:1,2:sv turn_dz:6 quantise_by_token:6 quantise_w:5 sum_vector:7,0 copy_dz:6:ss "
    "half_sum:1,0:ss weight_gradient:2,0:ss quantise_by_feature:5 quantise_by_token:7 weight_gradient:2,3:sv "
    "turn_dz:7 quantise_w:6 weight_gradient:3,3:ss weight_gradient:3,0:ss quantise_by_feature:6 copy_dz:7:vs "
    "weight_gradient:3,1:vv quantise_w:7 quantise_w:4 weight_gradient:2,2:ss quantise_by_feature:7 "
    "weight_gradient:3,2:ss input_gradient:0,1 input_gradient:1,2 input_gradient:0,2 input_gradient:0,3 "
    "input_gradient:1,3 input_gradient:1,0 input_gradient:1,1 input_gradient:0,0:halves",
)


def tile_selfattention_pa_v_kernel(tc, x, wq, bq, wk, bk, grad_0, grad_1, out_0, out_1, out_2):
    nc = tc.nc
    x_rows = x.rearrange("b s f -> (b s) f").rearrange("(g p t) f -> g p t f", p=P, t=PACK)
    grad_rows = [
        grad.rearrange("b s h d -> (b s) (h d)").rearrange("(g p t) c -> g p t c", p=P, t=PACK)
        for grad in (grad_0, grad_1)
    ]
    w_rows = [w.rearrange("f h d -> f (h d)").rearrange("(z a p) c -> z p a c", z=2, p=P) for w in (wq, wk)]
    out_0_rows = out_0.rearrange("b s f -> (b s) f").rearrange("(g p t) (z f) -> g t p z f", p=P, t=PACK, z=2)
    dw_rows = [
        out.rearrange("f h d -> f (h d)").rearrange("(m a p) (k c) -> m k p a c", a=2, p=P, k=2) for out in (out_1, out_2)
    ]

    with ExitStack() as ctx:
        const = ctx.enter_context(tc.tile_pool(name="const", bufs=1))
        inputs = ctx.enter_context(tc.tile_pool(name="inputs", bufs=1))
        operands = ctx.enter_context(tc.tile_pool(name="operands", bufs=1))
        work = ctx.enter_context(tc.tile_pool(name="work", bufs=2))
        results = ctx.enter_context(tc.tile_pool(name="results", bufs=6))
        table_banks = ctx.enter_context(tc.psum_pool(name="table_banks", bufs=1))
        turn_banks = ctx.enter_context(tc.psum_pool(name="turn_banks", bufs=2))
        sum_banks = ctx.enter_context(tc.psum_pool(name="sum_banks", bufs=4))
        ctx.enter_context(tc.manual_schedule())

        grad_tile, x_tile, w_tile = {}, {}, {}

        def load_grad_0(g, k):
            tile = inputs.tile([P, PACK, PASS], BF16, name=f"grad_{g}{k}", align_bytes=64)
            nc.sync.dma_start(out=tile[:], in_=grad_rows[0][g][:, :, PASS * k : PASS * (k + 1)])
            grad_tile[g, k] = tile

        def load_grad_1(g):
            for k in (2, 3):
                tile = inputs.tile([P, PACK, PASS], BF16, name=f"x_{g}{k - 2}", align_bytes=64)
                nc.sync.dma_start(out=tile[:], in_=grad_rows[1][g][:, :, PASS * (k - 2) : PASS * (k - 1)])
                grad_tile[g, k] = tile

        def load_x(g, z):
            tile = inputs.tile([P, PACK, PASS], BF16, name=f"x_{g}{z}", align_bytes=64)
            nc.sync.dma_start(out=tile[:], in_=x_rows[g][:, :, PASS * z : PASS * (z + 1)])
            x_tile[g, z] = tile

        def load_w(layer, z):
            tile = inputs.tile([P, PACK, OUT_FEATURES], BF16, name=f"w_{z}", align_bytes=64)
            nc.sync.dma_start(out=tile[:], in_=w_rows[layer][z])
            w_tile[layer, z] = tile

        def load_wk(z):
            load_w(1, z)

        load_x(0, 0)
        load_grad_0(0, 0)
        load_x(0, 1)
        load_grad_0(1, 0)
        load_x(1, 0)
        load_x(1, 1)
        load_grad_0(0, 1)
        load_w(0, 0)
        load_w(0, 1)
        load_grad_0(1, 1)

        row_number = const.tile([P, 1], I32)
        nc.gpsimd.iota(row_number[:], pattern=[[0, 1]], base=0, channel_multiplier=1)
        position = const.tile([P, POSITIONS], F32)
        nc.gpsimd.iota(
            position[:],
            pattern=[[1, PACK], [PACK, ROUNDS]],
            base=0,
            channel_multiplier=0,
            allow_small_or_imprecise_dtypes=True,
        )
        identity = const.tile([P, P], F32)
        make_identity(nc, identity[:])
        bits = const.tile([P, 7], I32)
        for b in range(7):
            nc.vector.tensor_scalar(
                out=bits[:, b : b + 1],
                in0=row_number[:],
                scalar1=b,
                scalar2=1,
                op0=ALU.logical_shift_right,
                op1=ALU.bitwise_and,
            )
        factors = const.tile([P, 6], F32)
        for b in range(6):
            nc.vector.tensor_scalar(
                out=factors[:, b : b + 1],
                in0=bits[:, b : b + 1],
                scalar1=THETA ** (-(2.0**b) / HALF) - 1.0,
                scalar2=1.0,
                op0=ALU.mult,
                op1=ALU.add,
            )
        phase = const.tile([P, 1], F32)
        nc.vector.tensor_scalar(
            out=phase[:], in0=bits[:, 6:7], scalar1=-0.25, scalar2=0.25, op0=ALU.mult, op1=ALU.add
        )
        triples = const.tile([P, 3], F32)
        nc.vector.tensor_tensor(out=triples[:], in0=factors[:, 0:3], in1=factors[:, 3:6], op=ALU.mult)
        pair = const.tile([P, 1], F32)
        nc.vector.tensor_tensor(out=pair[:], in0=triples[:, 0:1], in1=triples[:, 1:2], op=ALU.mult)
        turns_per_step = const.tile([P, 1], F32)
        nc.vector.scalar_tensor_tensor(
            out=turns_per_step[:],
            in0=pair[:],
            scalar=0.5 / math.pi,
            in1=triples[:, 2:3],
            op0=ALU.mult,
            op1=ALU.mult,
        )
        turns = const.tile([P, POSITIONS], F32)
        nc.vector.tensor_scalar(
            out=turns[:], in0=position[:], scalar1=turns_per_step[:], scalar2=phase[:], op0=ALU.mult, op1=ALU.add
        )
        whole_turns = const.tile([P, POSITIONS], I32)
        nc.vector.tensor_copy(out=whole_turns[:], in_=turns[:])
        rest = const.tile([P, PACK, ROUNDS], F32)
        nc.vector.tensor_tensor(
            out=rest[:].rearrange("q t s -> q (t s)"), in0=turns[:], in1=whole_turns[:], op=ALU.subtract
        )
        tables = []
        for sign in (1.0, -1.0):
            wave = const.tile([P, PACK, 2, ROUNDS], F32, name="wave", bufs=2)
            nc.scalar.activation(
                out=wave[:],
                in_=rest[:].unsqueeze(2).to_broadcast([P, PACK, 2, ROUNDS]),
                func=ACT.Sin,
                scale=sign * 2.0 * math.pi,
            )
            table = table_banks.tile([P, PACK, P], F32, name="table" if sign > 0 else "negative_table")
            for t in range(PACK):
                nc.tensor.transpose(table[:, t, :], wave[:, t, :, :].rearrange("q a s -> q (a s)"), identity[:])
            tables.append(table)
        cosine = tables[0][:, :, 0:HALF].unsqueeze(2)
        sine = tables[0][:, :, HALF:P].unsqueeze(2)
        minus_sine = tables[1][:, :, HALF:P].unsqueeze(2)

        product_tiles, dz = {}, {}

        def products(u):
            grad = grad_tile[UNITS[u]][:].rearrange("p t (q j) -> p t q j", j=HALF)
            straight = work.tile([P, PACK, HALVES, HALF], F32, name="straight", align_bytes=64)
            nc.vector.tensor_tensor(
                out=straight[:], in0=grad, in1=cosine.to_broadcast([P, PACK, HALVES, HALF]), op=ALU.mult
            )
            crossed = work.tile([P, PACK, HALVES, HALF], F32, name="crossed", align_bytes=64)
            for to_half, table in ((0, sine), (1, minus_sine)):
                nc.vector.tensor_tensor(
                    out=crossed[:, :, to_half:HALVES:2, :],
                    in0=grad[:, :, 1 - to_half : HALVES : 2, :],
                    in1=table.to_broadcast([P, PACK, HALVES // 2, HALF]),
                    op=ALU.mult,
                )
            product_tiles[u] = (straight, crossed)
            if u == len(UNITS) - 1:
                bank_cycle.extend(
                    [(sum_banks, "sum"), (table_banks, "table"), (sum_banks, "sum"), (table_banks, "negative_table")]
                )

        def sum_columns(u, engine, first, last):
            if u not in dz:
                tile = work.tile([P, PASS, PACK], BF16, name="dz", bufs=1, align_bytes=64)
                dz[u] = tile
            terms = [
                tile[:].rearrange("p t q j -> p t (q j)")[:, :, first:last].rearrange("p t (c r) -> p c t r", r=RUN)
                for tile in product_tiles[u]
            ]
            engine.tensor_tensor(
                out=dz[u][:, first:last, :].rearrange("p (c r) t -> p c t r", r=RUN),
                in0=terms[0],
                in1=terms[1],
                op=ALU.add,
            )

        def sum_gpsimd(u, columns):
            sum_columns(u, nc.gpsimd, 0, columns)

        def sum_vector(u, columns):
            sum_columns(u, nc.vector, columns, PASS)

        dz_by_token, dz_by_feature, x_by_token, w_by_feature = {}, {}, {}, {}

        def quantise(tile, fmt, name):
            codes = operands.tile([P, PASS], U32, name=f"{name}_codes", align_bytes=64)
            scales = operands.tile([P, PASS], U8, name=f"{name}_scales", align_bytes=64)
            nc.vector.quantize_mx(
                out=codes[:].bitcast(fmt), scales=scales[:], in_=tile[:].rearrange("p c i -> p (c i)")
            )
            return codes, scales

        def move(engine, out, in_):
            copy = nc.vector.tensor_copy if engine == "v" else nc.scalar.copy
            copy(out=out, in_=in_)

        def quantise_by_token(u):
            g, k = UNITS[u]
            dz_by_token[g, k] = quantise(dz[u], E5M2, f"dz_by_token_{g}{k}")

        turned, dz_turned = {}, {}

        def turn_dz(u):
            words = dz[u][:].rearrange("p c t -> p (c t)").bitcast(F32)
            for h in range(2):
                bank = turn_banks.tile([P, PACK, P], F32, name="turn")
                for i in range(PACK):
                    nc.tensor.transpose(bank[:, i, :], words[:, 2 * i + h : 2 * PASS : 2 * PACK], identity[:])
                turned[u, h] = bank

        def copy_dz(u, engines):
            tile = work.tile([P, PASS, PACK], BF16, name="dz_turned", align_bytes=64)
            for h in range(2):
                move(
                    engines[h],
                    tile[:, 2 * P * h : 2 * P * (h + 1), :].rearrange("p (e n) i -> p e n i", e=2),
                    turned[u, h][:]
                    .rearrange("p i n -> p (i n)")
                    .bitcast(BF16)
                    .rearrange("p (i n e) -> p e n i", i=PACK, e=2),
                )
            dz_turned[u] = tile

        def quantise_by_feature(u):
            g, k = UNITS[u]
            dz_by_feature[g, k] = quantise(dz_turned[u], E5M2, f"dz_by_feature_{g}{k % 2}")

        x_laid, w_laid = {}, {}

        def copy_x(g, z):
            tile = work.tile([P, PASS, PACK], BF16, name="laid", bufs=4, align_bytes=64)
            nc.scalar.copy(
                out=tile[:].rearrange("p (c r) t -> p c t r", r=RUN),
                in_=x_tile[g, z][:].rearrange("p t (c r) -> p c t r", r=RUN),
            )
            x_laid[g, z] = tile

        def quantise_x(g, z):
            x_by_token[g, z] = quantise(x_laid[g, z], E4M3, f"x_by_token_{g}{z}")

        def turn_w(n):
            k, z = W_PIECES[n]
            words = w_tile[k // 2, z][:].rearrange("p a c -> p (a c)").bitcast(F32)
            for y in range(2):
                bank = turn_banks.tile([P, 2, 2, P], F32, name="turn")
                for a in range(2):
                    first = OUT_FEATURES // 2 * (2 * y + a) + PASS // 2 * (k % 2)
                    for u in range(2):
                        nc.tensor.transpose(bank[:, a, u, :], words[:, first + u : first + PASS // 2 : 2], identity[:])
                turned["w", n, y] = bank

        def copy_w(n, engines):
            tile = work.tile([P, PASS, PACK], BF16, name="laid", bufs=4, align_bytes=64)
            words = tile[:].rearrange("p c i -> p (c i)").bitcast(F32)
            for y in range(2):
                move(
                    engines[y],
                    words[:, PASS * y : PASS * (y + 1)].rearrange("p (a f u) -> p a f u", a=2, u=2),
                    turned["w", n, y][:].rearrange("p a u f -> p a f u"),
                )
            w_laid[n] = tile

        def quantise_w(n):
            k, z = W_PIECES[n]
            w_by_feature[k, z] = quantise(w_laid[n], E4M3, f"w_by_feature_{k}{z}")

        bank_cycle = [(sum_banks, "sum")]
        banks_taken = [0]

        def new_bank():
            pool, name = bank_cycle[banks_taken[0] % len(bank_cycle)]
            banks_taken[0] += 1
            bank = pool.tile([P, PASS], F32, name=name)
            return bank

        def multiply(bank, stationary, column, stationary_fmt, moving, moving_fmt, start, stop):
            nc.tensor.matmul_mx(
                out=bank[:],
                lhsT=stationary[0][:, column : column + P].bitcast(stationary_fmt),
                lhsT_scale=stationary[1][:, column : column + P],
                rhs=moving[0][:].bitcast(moving_fmt),
                rhs_scale=moving[1][:],
                start=start,
                stop=stop,
            )

        def weight_gradient(k, m, engines):
            result = results.tile([P, 2, PASS], F32, name="result")
            for a in range(2):
                bank = new_bank()
                f = P * (2 * m + a)
                for g in range(2):
                    multiply(bank, x_by_token[g, f // PASS], f % PASS, E4M3, dz_by_token[g, k], E5M2, g == 0, g == 1)
                move(engines[a], result[:, a, :], bank[:])
            nc.sync.dma_start(out=dw_rows[k // 2][m][k % 2], in_=result[:])

        half_sums = {}

        def dx_sum(g, t, z, blocks):
            bank = new_bank()
            for k in blocks:
                multiply(
                    bank, dz_by_feature[g, k], P * t, E5M2, w_by_feature[k, z], E4M3, k == blocks[0], k == blocks[-1]
                )
            return bank

        def half_sum(g, t, engines):
            kept = results.tile([P, 2, PASS], F32, name=f"half_sum_{g}{t}", bufs=1)
            for z in range(2):
                bank = dx_sum(g, t, z, (0, 1))
                move(engines[z], kept[:, z, :], bank[:])
            half_sums[g, t] = kept

        def input_gradient(g, t, stores="whole"):
            result = results.tile([P, 2, PASS], F32, name="result")
            for z in range(2):
                bank = dx_sum(g, t, z, (2, 3))
                nc.vector.tensor_tensor(out=result[:, z, :], in0=bank[:], in1=half_sums[g, t][:, z, :], op=ALU.add)
            if stores == "halves":
                for z in range(2):
                    nc.sync.dma_start(out=out_0_rows[g][t][:, z, :], in_=result[:, z, :])
            else:
                nc.sync.dma_start(out=out_0_rows[g][t], in_=result[:])

        steps = {
            "load_grad_1": load_grad_1,
            "load_wk": load_wk,
            "products": products,
            "sum_gpsimd": sum_gpsimd,
            "sum_vector": sum_vector,
            "turn_dz": turn_dz,
            "copy_dz": copy_dz,
            "quantise_by_token": quantise_by_token,
            "quantise_by_feature": quantise_by_feature,
            "copy_x": copy_x,
            "quantise_x": quantise_x,
            "turn_w": turn_w,
            "copy_w": copy_w,
            "quantise_w": quantise_w,
            "weight_gradient": weight_gradient,
            "half_sum": half_sum,
            "input_gradient": input_gradient,
        }
        for line in ORDER:
            for step in line.split():
                parts = step.split(":")
                steps[parts[0]](*[int(number) for number in parts[1].split(",")], *parts[2:])
